import numpy as np
import ml_dtypes


def mxq(x, axis, fmt="e4m3"):
    dtype, down = {"e4m3": (ml_dtypes.float8_e4m3fn, 7), "e5m2": (ml_dtypes.float8_e5m2, 14)}[fmt]
    v = np.moveaxis(np.asarray(x, np.float32).astype(ml_dtypes.bfloat16).astype(np.float64), axis, -1)
    blocks = v.reshape(v.shape[:-1] + (-1, 32))
    amax = np.abs(blocks).max(-1, keepdims=True)
    byte = np.maximum(np.where(amax > 0, np.frexp(amax)[1] - 1 + 127, 0) - down, 1)
    scale = np.exp2(byte - 127.0)
    codes = (blocks / scale).astype(np.float32).astype(dtype).astype(np.float64)
    return np.moveaxis((codes * scale).reshape(v.shape), -1, axis)


WIDE = False


def mx_kscale(k):
    if not WIDE:
        return np.ones(k)
    levels = np.array([10, -10, 5, -5, 0])
    a = np.random.permutation(np.resize(levels, k // 512 * 4)).reshape(k // 512, 4)
    idx = np.arange(k)
    return np.exp2(a[idx // 512, idx % 128 // 32])


BF16 = ml_dtypes.bfloat16


def bf(x):
    return np.asarray(x, np.float32).astype(BF16)


def f64(x):
    return np.asarray(x).astype(np.float64)


E2M1 = np.array([0.0, 0.5, 1.0, 1.5, 2.0, 3.0, 4.0, 6.0, -0.0, -0.5, -1.0, -1.5, -2.0, -3.0, -4.0, -6.0])


def pack_weight(w, fmt):
    k, n = w.shape
    w = f64(bf(w)).reshape(k // 32, 32, n)
    amax = np.abs(w).max(1)
    if fmt == "e4m3":
        byte = np.frexp(amax)[1] - 1 + 127 - 7
    else:
        mant, ex = np.frexp(amax / 6.0)
        byte = np.where(mant > 0.5, ex, ex - 1) + 127
    byte = np.clip(np.where(amax > 0, byte, 1), 1, 254)
    scaled = (w * np.exp2(127.0 - byte)[:, None, :]).reshape(k, n).astype(np.float32)
    by_word = np.ascontiguousarray(scaled.reshape(k // 512, 128, 4, n).transpose(0, 1, 3, 2))
    if fmt == "e4m3":
        words = by_word.astype(ml_dtypes.float8_e4m3fn).view(np.uint8)
    else:
        c = by_word.astype(ml_dtypes.float4_e2m1fn).view(np.uint8) & 0xF
        words = c[..., 0::2] | (c[..., 1::2] << 4)
    return np.ascontiguousarray(words), np.ascontiguousarray(byte.astype(np.uint8).reshape(k // 512, 16, n))


def unpack_weight(words, scales, fmt):
    g, p, n, _ = words.shape
    if fmt == "e4m3":
        vals = np.ascontiguousarray(words).view(ml_dtypes.float8_e4m3fn).astype(np.float64)
    else:
        nib = np.empty((g, p, n, 4), np.uint8)
        nib[..., 0::2] = words & 0xF
        nib[..., 1::2] = words >> 4
        vals = E2M1[nib]
    vals = vals * np.repeat(np.exp2(scales.astype(np.float64) - 127.0), 8, axis=1)[..., None]
    return vals.transpose(0, 1, 3, 2).reshape(g * 512, n)


B, C, N, W, H = 2, 512, 512, 32, 32
M = W * H
SIGMA = 3.0
FMT = "e4m3"


def setup_inputs():
    t = mx_kscale(C)
    a = np.sqrt(SIGMA) * C ** -0.25
    q = bf(np.random.standard_normal((B, N, C)) * a)
    k = bf(np.random.standard_normal((B, M, C)) * a)
    v = bf(np.random.standard_normal((B, M, C)) * 8.0 * t)
    Wo = np.random.standard_normal((C, C)) * 0.25 / t
    Wo_words, Wo_scales = pack_weight(Wo.T, FMT)
    bo = bf(np.random.standard_normal(C) * 0.2)
    feat0 = bf(np.random.standard_normal((B, C, N)))
    return {"q": q,
            "k": k,
            "v": v,
            "Wo_words": Wo_words,
            "Wo_scales": Wo_scales,
            "bo": bo,
            "feat0": feat0}


def reference(q, k, v, Wo_words, Wo_scales, bo, feat0):
    energy = f64(q) @ f64(k).transpose(0, 2, 1)
    e = np.exp(energy - energy.max(-1, keepdims=True))
    ctx = (mxq(e, 2, "e4m3") @ mxq(f64(v), 1, "e4m3")) / e.sum(-1, keepdims=True) * C ** -0.5
    y = (mxq(ctx, 2, "e4m3") @ unpack_weight(Wo_words, Wo_scales, FMT)) + f64(bo)
    return y.transpose(0, 2, 1) + f64(feat0)

@@ -1,0 +1,292 @@
+import math
+from contextlib import ExitStack
+
+import concourse.mybir as mybir
+from concourse.masks import make_identity
+
+F32 = mybir.dt.float32
+BF16 = mybir.dt.bfloat16
+I32 = mybir.dt.int32
+U32 = mybir.dt.uint32
+U8 = mybir.dt.uint8
+FP8X4 = mybir.dt.float8_e4m3fn_x4
+ALU = mybir.AluOpType
+ACT = mybir.ActivationFunctionType
+AXIS = mybir.AxisListType
+
+P = 128
+PACK = 4
+BANK = 512
+BATCH, POINTS, POSITIONS, CHANNELS = 2, 512, 1024, 512
+POINT_TILES = POINTS // P
+STEPS = BATCH * POINT_TILES
+HALVES = POSITIONS // BANK
+PASSES = POSITIONS // (P * PACK)
+OUT_TILES = CHANNELS // P
+CHUNK = 2 * P
+PAIR = 2 * P
+HEAD_CHUNKS = 3
+PV_LAG = 2
+FLOPS = 2 * BATCH * (2 * POINTS * POSITIONS * CHANNELS + POINTS * CHANNELS * CHANNELS)
+
+
+def tile_i2p_crossattention_pa_kernel(tc, q, k, v, Wo_words, Wo_scales, bo, feat0, out):
+    nc = tc.nc
+    with ExitStack() as ctx:
+        ctx.enter_context(tc.manual_schedule())
+        keep = ctx.enter_context(tc.tile_pool(name="keep", bufs=1))
+        small = ctx.enter_context(tc.tile_pool(name="small", bufs=3))
+        work = ctx.enter_context(tc.tile_pool(name="work", bufs=2))
+        lagged = ctx.enter_context(tc.tile_pool(name="lagged", bufs=PV_LAG + 2))
+        energy_psum = ctx.enter_context(tc.psum_pool(name="energy_psum", bufs=3))
+        transpose_psum = ctx.enter_context(tc.psum_pool(name="transpose_psum", bufs=3))
+        mx_psum = ctx.enter_context(tc.psum_pool(name="mx_psum", bufs=2))
+
+        identity = keep.tile([P, P], F32, name="identity")
+        ones = keep.tile([P, P], F32, name="ones")
+        bias_rows = keep.tile([P, P], BF16, name="bias_rows")
+        bias_rows_f32 = keep.tile([P, P], F32, name="bias_rows_f32")
+        bias = keep.tile([P, OUT_TILES], F32, name="bias")
+        w_codes = keep.tile([P, CHANNELS], U32, name="w_codes", align_bytes=64)
+        w_scales = keep.tile([P, CHANNELS], U8, name="w_scales", align_bytes=64)
+        q_rows, k_rows, v_rows, feat, q_t, k_t, v_codes, v_scales = [], [], [], [], [], [], [], []
+        for b in range(BATCH):
+            q_rows.append(keep.tile([P, POINTS // P, CHANNELS], BF16, name="q_rows%d" % b))
+            k_rows.append(keep.tile([P, POSITIONS // P, CHANNELS], BF16, name="k_rows%d" % b))
+            feat.append(keep.tile([P, OUT_TILES, POINTS], BF16, name="feat%d" % b))
+            v_rows.append(keep.tile([P, PASSES, PACK, CHANNELS], BF16, name="v_rows%d" % b))
+            q_t.append(keep.tile([P, 2, 2 * POINTS], BF16, name="q_t%d" % b))
+            k_t.append(keep.tile([P, 2, 2 * POSITIONS], BF16, name="k_t%d" % b))
+            v_codes.append(keep.tile([P, PASSES, CHANNELS], U32, name="v_codes%d" % b, align_bytes=64))
+            v_scales.append(keep.tile([P, PASSES, CHANNELS], U8, name="v_scales%d" % b, align_bytes=64))
+
+        nc.vector.memset(w_scales[:].bitcast(I32), 0)
+        nc.vector.memset(bias_rows[:], 0.0)
+        make_identity(nc, identity[:])
+        nc.gpsimd.memset(ones[:], 1.0)
+
+        def load_chunk(rows, source, chunk):
+            tiles = slice(2 * chunk, 2 * chunk + 2)
+            nc.sync.dma_start(out=rows[:, tiles, :], in_=source.rearrange("(a p) c -> p a c", p=P)[:, tiles, :])
+
+        def load_q_and_k(b):
+            load_chunk(q_rows[b], q[b], 0)
+            for chunk in range(POSITIONS // CHUNK):
+                load_chunk(k_rows[b], k[b], chunk)
+            load_chunk(q_rows[b], q[b], 1)
+
+        def load_v(b):
+            for g in range(PASSES):
+                positions = slice(g * P * PACK, (g + 1) * P * PACK)
+                nc.sync.dma_start(
+                    out=v_rows[b][:, g].rearrange("p (u j) c -> p u (j c)", j=2),
+                    in_=v[b, positions, :].rearrange("(u p j) c -> p u (j c)", u=2, j=2),
+                )
+
+        def load_feat(b):
+            nc.sync.dma_start(out=feat[b][:], in_=feat0[b].rearrange("(o p) n -> p o n", p=P))
+
+        nc.sync.dma_start(out=bias_rows[0:OUT_TILES, :], in_=bo.rearrange("(o p) -> o p", p=P))
+        load_q_and_k(0)
+        load_v(0)
+        load_q_and_k(1)
+        nc.sync.dma_start(out=w_codes[:].bitcast(I32), in_=Wo_words[0].rearrange("p n t -> p (n t)").bitcast(I32))
+        for quadrant in range(4):
+            nc.sync.dma_start(
+                out=w_scales[32 * quadrant : 32 * quadrant + 4, :].bitcast(I32),
+                in_=Wo_scales[0, 4 * quadrant : 4 * quadrant + 4, :].bitcast(I32),
+            )
+        load_feat(0)
+        load_v(1)
+        load_feat(1)
+
+        nc.vector.tensor_copy(out=bias_rows_f32[:], in_=bias_rows[:])
+        bias_bank = transpose_psum.tile([P, P], F32, name="bias_bank", tag="transposes")
+        nc.tensor.transpose(bias_bank[:], bias_rows_f32[:], identity[:])
+        nc.vector.tensor_copy(out=bias[:], in_=bias_bank[:, 0:OUT_TILES])
+
+        energy_banks, row_max, row_sums, e_rows, spread = {}, {}, {}, {}, {}
+        e_codes, e_scales, inv_cols, v_grouped, ctx_codes, ctx_scales = {}, {}, {}, {}, {}, {}
+
+        def transpose_chunk(rows, transposed, chunk):
+            bank = transpose_psum.tile([P, 2, CHUNK], F32, name="chunk_bank", tag="transposes")
+            for a in range(2):
+                words = rows[:, 2 * chunk + a, :].bitcast(F32)
+                for w in range(2):
+                    nc.tensor.transpose(bank[:, w, a * P : (a + 1) * P], words[:, w * P : (w + 1) * P], identity[:])
+            nc.scalar.copy(out=transposed[:].bitcast(F32)[:, :, chunk * CHUNK : (chunk + 1) * CHUNK], in_=bank[:])
+
+        def energy(s, h):
+            b, i = divmod(s, POINT_TILES)
+            q_view = q_t[b][:].rearrange("p w (r j) -> p w r j", j=2)
+            k_view = k_t[b][:].rearrange("p w (r j) -> p w r j", j=2)
+            bank = energy_psum.tile([P, BANK], F32, name="energy_bank", tag="energy")
+            for c in range(4):
+                w, j = divmod(c, 2)
+                nc.tensor.matmul(
+                    bank[:],
+                    lhsT=q_view[:, w, i * P : (i + 1) * P, j],
+                    rhs=k_view[:, w, h * BANK : (h + 1) * BANK, j],
+                    start=(c == 0),
+                    stop=(c == 3),
+                )
+            if h == 0:
+                row_max[s] = small.tile([P, HALVES], F32, name="row_max")
+            nc.vector.reduce_max(out=row_max[s][:, h : h + 1], in_=bank[:], axis=AXIS.X)
+            energy_banks[(s, h)] = bank
+
+        def exponentials(s):
+            neg_max = small.tile([P, 1], F32, name="neg_max")
+            nc.vector.tensor_scalar(
+                out=neg_max[:], in0=row_max[s][:, 0:1], scalar1=row_max[s][:, 1:2], scalar2=-1.0,
+                op0=ALU.max, op1=ALU.mult,
+            )
+            e_rows[s] = work.tile([P, POSITIONS], BF16, name="e_rows")
+            row_sums[s] = small.tile([P, HALVES], F32, name="row_sums")
+            for h in range(HALVES):
+                nc.scalar.activation(
+                    out=e_rows[s][:, h * BANK : (h + 1) * BANK], in_=energy_banks[(s, h)][:], func=ACT.Exp,
+                    bias=neg_max[:], scale=1.0, accum_out=row_sums[s][:, h : h + 1],
+                )
+
+        def denominator(s):
+            scaled_sum = small.tile([P, 1], F32, name="scaled_sum")
+            nc.vector.tensor_scalar(
+                out=scaled_sum[:], in0=row_sums[s][:, 0:1], scalar1=row_sums[s][:, 1:2],
+                scalar2=math.sqrt(CHANNELS), op0=ALU.add, op1=ALU.mult,
+            )
+            inverse = small.tile([P, 1], F32, name="inverse")
+            nc.vector.reciprocal(out=inverse[:], in_=scaled_sum[:])
+            spread[s] = work.tile([P, P], F32, name="spread")
+            nc.gpsimd.tensor_scalar(
+                out=spread[s][:], in0=ones[:], scalar1=inverse[:, 0:1], scalar2=0.0, op0=ALU.mult, op1=ALU.add
+            )
+
+        def transpose_e(s):
+            bank = transpose_psum.tile([P, PASSES, 2, P], F32, name="e_bank", tag="transposes")
+            words = e_rows[s][:].bitcast(F32)
+            for c in range(2 * PASSES):
+                g, u = divmod(c, 2)
+                nc.tensor.transpose(bank[:, g, u, :], words[:, c * P : (c + 1) * P], identity[:])
+            inv_bank = transpose_psum.tile([P, P], F32, name="inv_bank", tag="transposes")
+            nc.tensor.transpose(inv_bank[:], spread[s][:], identity[:])
+            grouped = work.tile([P, PASSES, PACK * P], BF16, name="e_grouped", align_bytes=64)
+            nc.scalar.copy(
+                out=grouped[:].bitcast(F32).rearrange("p g (n u) -> p g n u", u=2),
+                in_=bank[:].rearrange("p g u n -> p g n u"),
+            )
+            inv_cols[s] = lagged.tile([P, P], F32, name="inv_cols")
+            nc.scalar.copy(out=inv_cols[s][:], in_=inv_bank[:])
+            e_codes[s] = lagged.tile([P, PASSES, P], U32, name="e_codes", align_bytes=64)
+            e_scales[s] = lagged.tile([P, PASSES, P], U8, name="e_scales", align_bytes=64)
+            nc.vector.quantize_mx(
+                out=e_codes[s][:].rearrange("p g n -> p (g n)").bitcast(FP8X4),
+                scales=e_scales[s][:].rearrange("p g n -> p (g n)"),
+                in_=grouped[:].rearrange("p g c -> p (g c)"),
+            )
+
+        def regroup_v(b, g):
+            v_grouped[(b, g)] = work.tile([P, PACK, P, PACK], BF16, name="v_grouped", align_bytes=64)
+            source = v_rows[b][:, g].rearrange("p row (i t) -> p i row t", t=PACK)
+            target = v_grouped[(b, g)][:].rearrange("p t i row -> p i row t")
+            nc.vector.tensor_copy(out=target[:, 0 : P // 2], in_=source[:, 0 : P // 2])
+            nc.scalar.copy(out=target[:, P // 2 : P], in_=source[:, P // 2 : P])
+
+        def quantise_v(b, g):
+            nc.vector.quantize_mx(
+                out=v_codes[b][:, g, :].bitcast(FP8X4),
+                scales=v_scales[b][:, g, :],
+                in_=v_grouped[(b, g)][:].rearrange("p t i row -> p (t i row)"),
+            )
+
+        def attend(s):
+            b = s // POINT_TILES
+            bank = mx_psum.tile([P, PACK, P], F32, name="ctx_bank", tag="mx")
+            for t in range(PACK):
+                channels = slice(t * P, (t + 1) * P)
+                for g in range(PASSES):
+                    nc.tensor.matmul_mx(
+                        out=bank[:, t, :],
+                        lhsT=v_codes[b][:, g, channels].bitcast(FP8X4),
+                        lhsT_scale=v_scales[b][:, g, channels],
+                        rhs=e_codes[s][:, g, :].bitcast(FP8X4),
+                        rhs_scale=e_scales[s][:, g, :],
+                        start=(g == 0),
+                        stop=(g == PASSES - 1),
+                    )
+            grouped = work.tile([P, P, PACK], BF16, name="ctx_grouped", align_bytes=64)
+            nc.vector.tensor_tensor(
+                out=grouped[:],
+                in0=bank[:].rearrange("p t n -> p n t"),
+                in1=inv_cols[s][:].unsqueeze(2).to_broadcast([P, P, PACK]),
+                op=ALU.mult,
+            )
+            pair, member = divmod(s, 2)
+            if member == 0:
+                ctx_codes[pair] = work.tile([P, PAIR], U32, name="ctx_codes", align_bytes=64)
+                ctx_scales[pair] = work.tile([P, PAIR], U8, name="ctx_scales", align_bytes=64)
+            points = slice(member * P, (member + 1) * P)
+            nc.vector.quantize_mx(
+                out=ctx_codes[pair][:, points].bitcast(FP8X4),
+                scales=ctx_scales[pair][:, points],
+                in_=grouped[:].rearrange("p n t -> p (n t)"),
+            )
+
+        def project(pair, part):
+            b, place = divmod(pair, POINTS // PAIR)
+            points = slice(place * PAIR, (place + 1) * PAIR)
+            bank = mx_psum.tile([P, 2, PAIR], F32, name="y_bank", tag="mx")
+            result = work.tile([P, 2, PAIR], F32, name="result")
+            for c in range(2):
+                o = 2 * part + c
+                nc.tensor.matmul_mx(
+                    out=bank[:, c, :],
+                    lhsT=w_codes[:, o * P : (o + 1) * P].bitcast(FP8X4),
+                    lhsT_scale=w_scales[:, o * P : (o + 1) * P],
+                    rhs=ctx_codes[pair][:].bitcast(FP8X4),
+                    rhs_scale=ctx_scales[pair][:],
+                    start=True,
+                    stop=True,
+                )
+            for c in range(2):
+                o = 2 * part + c
+                nc.vector.scalar_tensor_tensor(
+                    out=result[:, c, :], in0=bank[:, c, :], scalar=bias[:, o : o + 1], in1=feat[b][:, o, points],
+                    op0=ALU.add, op1=ALU.add,
+                )
+            nc.sync.dma_start(
+                out=out[b].rearrange("(o p) n -> p o n", p=P)[:, 2 * part : 2 * part + 2, points], in_=result[:]
+            )
+
+        chunks = []
+        for b in range(BATCH):
+            chunks.append((q_rows[b], q_t[b], 0))
+            for chunk in range(POSITIONS // CHUNK):
+                chunks.append((k_rows[b], k_t[b], chunk))
+            chunks.append((q_rows[b], q_t[b], 1))
+
+        for rows, transposed, chunk in chunks[:HEAD_CHUNKS]:
+            transpose_chunk(rows, transposed, chunk)
+
+        for s in range(STEPS + PV_LAG + 2):
+            if 1 <= s <= STEPS:
+                denominator(s - 1)
+            if s < STEPS:
+                energy(s, 0)
+            first = HEAD_CHUNKS + 2 * s
+            for rows, transposed, chunk in chunks[first : first + 2]:
+                transpose_chunk(rows, transposed, chunk)
+            if 1 <= s <= STEPS:
+                transpose_e(s - 1)
+            b, i = divmod(s, POINT_TILES)
+            if b < BATCH and 1 <= i <= PASSES:
+                quantise_v(b, i - 1)
+            if s < STEPS:
+                energy(s, 1)
+                exponentials(s)
+            if 0 <= s - PV_LAG - 2 < STEPS:
+                project((s - PV_LAG - 2) // 2, (s - PV_LAG - 2) % 2)
+            if 0 <= s - PV_LAG < STEPS:
+                attend(s - PV_LAG)
+            if b < BATCH and i < PASSES:
+                regroup_v(b, i)

@@ -26,7 +26,8 @@ OUT_TILES = CHANNELS // P
 CHUNK = 2 * P
 PAIR = 2 * P
 HEAD_CHUNKS = 3
-PV_LAG = 2
+E_LAG = 2
+PV_LAG = 3
 FLOPS = 2 * BATCH * (2 * POINTS * POSITIONS * CHANNELS + POINTS * CHANNELS * CHANNELS)
 
 
@@ -35,12 +36,11 @@ def tile_i2p_crossattention_pa_kernel(tc, q, k, v, Wo_words, Wo_scales, bo, feat
     with ExitStack() as ctx:
         ctx.enter_context(tc.manual_schedule())
         keep = ctx.enter_context(tc.tile_pool(name="keep", bufs=1))
-        small = ctx.enter_context(tc.tile_pool(name="small", bufs=3))
+        small = ctx.enter_context(tc.tile_pool(name="small", bufs=E_LAG + 1))
         work = ctx.enter_context(tc.tile_pool(name="work", bufs=2))
-        lagged = ctx.enter_context(tc.tile_pool(name="lagged", bufs=PV_LAG + 2))
+        lagged = ctx.enter_context(tc.tile_pool(name="lagged", bufs=max(E_LAG, PV_LAG - E_LAG) + 1))
         energy_psum = ctx.enter_context(tc.psum_pool(name="energy_psum", bufs=3))
-        transpose_psum = ctx.enter_context(tc.psum_pool(name="transpose_psum", bufs=3))
-        mx_psum = ctx.enter_context(tc.psum_pool(name="mx_psum", bufs=2))
+        other_psum = ctx.enter_context(tc.psum_pool(name="other_psum", bufs=5))
 
         identity = keep.tile([P, P], F32, name="identity")
         ones = keep.tile([P, P], F32, name="ones")
@@ -101,20 +101,20 @@ def tile_i2p_crossattention_pa_kernel(tc, q, k, v, Wo_words, Wo_scales, bo, feat
         load_feat(1)
 
         nc.vector.tensor_copy(out=bias_rows_f32[:], in_=bias_rows[:])
-        bias_bank = transpose_psum.tile([P, P], F32, name="bias_bank", tag="transposes")
+        bias_bank = other_psum.tile([P, P], F32, name="bias_bank", tag="other")
         nc.tensor.transpose(bias_bank[:], bias_rows_f32[:], identity[:])
         nc.vector.tensor_copy(out=bias[:], in_=bias_bank[:, 0:OUT_TILES])
 
         energy_banks, row_max, row_sums, e_rows, spread = {}, {}, {}, {}, {}
-        e_codes, e_scales, inv_cols, v_grouped, ctx_codes, ctx_scales = {}, {}, {}, {}, {}, {}
+        e_grouped, e_codes, e_scales, inv_cols, v_grouped, ctx_codes, ctx_scales = {}, {}, {}, {}, {}, {}, {}
 
-        def transpose_chunk(rows, transposed, chunk):
-            bank = transpose_psum.tile([P, 2, CHUNK], F32, name="chunk_bank", tag="transposes")
+        def transpose_chunk(rows, transposed, chunk, copy):
+            bank = other_psum.tile([P, 2, CHUNK], F32, name="chunk_bank", tag="other")
             for a in range(2):
                 words = rows[:, 2 * chunk + a, :].bitcast(F32)
                 for w in range(2):
                     nc.tensor.transpose(bank[:, w, a * P : (a + 1) * P], words[:, w * P : (w + 1) * P], identity[:])
-            nc.scalar.copy(out=transposed[:].bitcast(F32)[:, :, chunk * CHUNK : (chunk + 1) * CHUNK], in_=bank[:])
+            copy(out=transposed[:].bitcast(F32)[:, :, chunk * CHUNK : (chunk + 1) * CHUNK], in_=bank[:])
 
         def energy(s, h):
             b, i = divmod(s, POINT_TILES)
@@ -141,7 +141,7 @@ def tile_i2p_crossattention_pa_kernel(tc, q, k, v, Wo_words, Wo_scales, bo, feat
                 out=neg_max[:], in0=row_max[s][:, 0:1], scalar1=row_max[s][:, 1:2], scalar2=-1.0,
                 op0=ALU.max, op1=ALU.mult,
             )
-            e_rows[s] = work.tile([P, POSITIONS], BF16, name="e_rows")
+            e_rows[s] = lagged.tile([P, POSITIONS], BF16, name="e_rows")
             row_sums[s] = small.tile([P, HALVES], F32, name="row_sums")
             for h in range(HALVES):
                 nc.scalar.activation(
@@ -163,26 +163,28 @@ def tile_i2p_crossattention_pa_kernel(tc, q, k, v, Wo_words, Wo_scales, bo, feat
             )
 
         def transpose_e(s):
-            bank = transpose_psum.tile([P, PASSES, 2, P], F32, name="e_bank", tag="transposes")
+            bank = other_psum.tile([P, PASSES, 2, P], F32, name="e_bank", tag="other")
             words = e_rows[s][:].bitcast(F32)
             for c in range(2 * PASSES):
                 g, u = divmod(c, 2)
                 nc.tensor.transpose(bank[:, g, u, :], words[:, c * P : (c + 1) * P], identity[:])
-            inv_bank = transpose_psum.tile([P, P], F32, name="inv_bank", tag="transposes")
+            inv_bank = other_psum.tile([P, P], F32, name="inv_bank", tag="other")
             nc.tensor.transpose(inv_bank[:], spread[s][:], identity[:])
-            grouped = work.tile([P, PASSES, PACK * P], BF16, name="e_grouped", align_bytes=64)
+            e_grouped[s] = work.tile([P, PASSES, PACK * P], BF16, name="e_grouped", align_bytes=64)
             nc.scalar.copy(
-                out=grouped[:].bitcast(F32).rearrange("p g (n u) -> p g n u", u=2),
+                out=e_grouped[s][:].bitcast(F32).rearrange("p g (n u) -> p g n u", u=2),
                 in_=bank[:].rearrange("p g u n -> p g n u"),
             )
             inv_cols[s] = lagged.tile([P, P], F32, name="inv_cols")
             nc.scalar.copy(out=inv_cols[s][:], in_=inv_bank[:])
+
+        def quantise_e(s):
             e_codes[s] = lagged.tile([P, PASSES, P], U32, name="e_codes", align_bytes=64)
             e_scales[s] = lagged.tile([P, PASSES, P], U8, name="e_scales", align_bytes=64)
             nc.vector.quantize_mx(
                 out=e_codes[s][:].rearrange("p g n -> p (g n)").bitcast(FP8X4),
                 scales=e_scales[s][:].rearrange("p g n -> p (g n)"),
-                in_=grouped[:].rearrange("p g c -> p (g c)"),
+                in_=e_grouped[s][:].rearrange("p g c -> p (g c)"),
             )
 
         def regroup_v(b, g):
@@ -201,7 +203,7 @@ def tile_i2p_crossattention_pa_kernel(tc, q, k, v, Wo_words, Wo_scales, bo, feat
 
         def attend(s):
             b = s // POINT_TILES
-            bank = mx_psum.tile([P, PACK, P], F32, name="ctx_bank", tag="mx")
+            bank = other_psum.tile([P, PACK, P], F32, name="ctx_bank", tag="other")
             for t in range(PACK):
                 channels = slice(t * P, (t + 1) * P)
                 for g in range(PASSES):
@@ -235,7 +237,7 @@ def tile_i2p_crossattention_pa_kernel(tc, q, k, v, Wo_words, Wo_scales, bo, feat
         def project(pair, part):
             b, place = divmod(pair, POINTS // PAIR)
             points = slice(place * PAIR, (place + 1) * PAIR)
-            bank = mx_psum.tile([P, 2, PAIR], F32, name="y_bank", tag="mx")
+            bank = other_psum.tile([P, 2, PAIR], F32, name="y_bank", tag="other")
             result = work.tile([P, 2, PAIR], F32, name="result")
             for c in range(2):
                 o = 2 * part + c
@@ -260,30 +262,33 @@ def tile_i2p_crossattention_pa_kernel(tc, q, k, v, Wo_words, Wo_scales, bo, feat
 
         chunks = []
         for b in range(BATCH):
-            chunks.append((q_rows[b], q_t[b], 0))
+            chunks.append((q_rows[b], q_t[b], 0, nc.scalar.copy))
             for chunk in range(POSITIONS // CHUNK):
-                chunks.append((k_rows[b], k_t[b], chunk))
-            chunks.append((q_rows[b], q_t[b], 1))
+                chunks.append((k_rows[b], k_t[b], chunk, nc.vector.tensor_copy if chunk % 2 == 0 else nc.scalar.copy))
+            chunks.append((q_rows[b], q_t[b], 1, nc.vector.tensor_copy))
 
-        for rows, transposed, chunk in chunks[:HEAD_CHUNKS]:
-            transpose_chunk(rows, transposed, chunk)
+        for rows, transposed, chunk, copy in chunks[:HEAD_CHUNKS]:
+            transpose_chunk(rows, transposed, chunk, copy)
 
         for s in range(STEPS + PV_LAG + 2):
-            if 1 <= s <= STEPS:
-                denominator(s - 1)
+            transposing = 0 <= s - E_LAG < STEPS
             if s < STEPS:
                 energy(s, 0)
             first = HEAD_CHUNKS + 2 * s
-            for rows, transposed, chunk in chunks[first : first + 2]:
-                transpose_chunk(rows, transposed, chunk)
-            if 1 <= s <= STEPS:
-                transpose_e(s - 1)
-            b, i = divmod(s, POINT_TILES)
-            if b < BATCH and 1 <= i <= PASSES:
-                quantise_v(b, i - 1)
+            for rows, transposed, chunk, copy in chunks[first : first + 2]:
+                transpose_chunk(rows, transposed, chunk, copy)
+            if transposing:
+                transpose_e(s - E_LAG)
             if s < STEPS:
                 energy(s, 1)
                 exponentials(s)
+            if 0 <= s + 1 - E_LAG < STEPS:
+                denominator(s + 1 - E_LAG)
+            if transposing:
+                quantise_e(s - E_LAG)
+            b, i = divmod(s, POINT_TILES)
+            if b < BATCH and 1 <= i <= PASSES:
+                quantise_v(b, i - 1)
             if 0 <= s - PV_LAG - 2 < STEPS:
                 project((s - PV_LAG - 2) // 2, (s - PV_LAG - 2) % 2)
             if 0 <= s - PV_LAG < STEPS:

@@ -25,9 +25,11 @@ PASSES = POSITIONS // (P * PACK)
 OUT_TILES = CHANNELS // P
 CHUNK = 2 * P
 PAIR = 2 * P
-HEAD_CHUNKS = 3
+HEAD_CHUNKS = 5
 E_LAG = 2
-PV_LAG = 3
+INV_LAG = 3
+PV_LAG = 4
+Y_LAG = 7
 FLOPS = 2 * BATCH * (2 * POINTS * POSITIONS * CHANNELS + POINTS * CHANNELS * CHANNELS)
 
 
@@ -38,9 +40,9 @@ def tile_i2p_crossattention_pa_kernel(tc, q, k, v, Wo_words, Wo_scales, bo, feat
         keep = ctx.enter_context(tc.tile_pool(name="keep", bufs=1))
         small = ctx.enter_context(tc.tile_pool(name="small", bufs=E_LAG + 1))
         work = ctx.enter_context(tc.tile_pool(name="work", bufs=2))
-        lagged = ctx.enter_context(tc.tile_pool(name="lagged", bufs=max(E_LAG, PV_LAG - E_LAG) + 1))
-        energy_psum = ctx.enter_context(tc.psum_pool(name="energy_psum", bufs=3))
-        other_psum = ctx.enter_context(tc.psum_pool(name="other_psum", bufs=5))
+        lagged = ctx.enter_context(tc.tile_pool(name="lagged", bufs=max(INV_LAG, PV_LAG - E_LAG) + 1))
+        energy_psum = ctx.enter_context(tc.psum_pool(name="energy_psum", bufs=4))
+        other_psum = ctx.enter_context(tc.psum_pool(name="other_psum", bufs=4))
 
         identity = keep.tile([P, P], F32, name="identity")
         ones = keep.tile([P, P], F32, name="ones")
@@ -157,7 +159,7 @@ def tile_i2p_crossattention_pa_kernel(tc, q, k, v, Wo_words, Wo_scales, bo, feat
             )
             inverse = small.tile([P, 1], F32, name="inverse")
             nc.vector.reciprocal(out=inverse[:], in_=scaled_sum[:])
-            spread[s] = work.tile([P, P], F32, name="spread")
+            spread[s] = lagged.tile([P, P], F32, name="spread")
             nc.gpsimd.tensor_scalar(
                 out=spread[s][:], in0=ones[:], scalar1=inverse[:, 0:1], scalar2=0.0, op0=ALU.mult, op1=ALU.add
             )
@@ -168,13 +170,15 @@ def tile_i2p_crossattention_pa_kernel(tc, q, k, v, Wo_words, Wo_scales, bo, feat
             for c in range(2 * PASSES):
                 g, u = divmod(c, 2)
                 nc.tensor.transpose(bank[:, g, u, :], words[:, c * P : (c + 1) * P], identity[:])
-            inv_bank = other_psum.tile([P, P], F32, name="inv_bank", tag="other")
-            nc.tensor.transpose(inv_bank[:], spread[s][:], identity[:])
             e_grouped[s] = work.tile([P, PASSES, PACK * P], BF16, name="e_grouped", align_bytes=64)
             nc.scalar.copy(
                 out=e_grouped[s][:].bitcast(F32).rearrange("p g (n u) -> p g n u", u=2),
                 in_=bank[:].rearrange("p g u n -> p g n u"),
             )
+
+        def transpose_inverse(s):
+            inv_bank = other_psum.tile([P, P], F32, name="inv_bank", tag="other")
+            nc.tensor.transpose(inv_bank[:], spread[s][:], identity[:])
             inv_cols[s] = lagged.tile([P, P], F32, name="inv_cols")
             nc.scalar.copy(out=inv_cols[s][:], in_=inv_bank[:])
 
@@ -225,8 +229,8 @@ def tile_i2p_crossattention_pa_kernel(tc, q, k, v, Wo_words, Wo_scales, bo, feat
             )
             pair, member = divmod(s, 2)
             if member == 0:
-                ctx_codes[pair] = work.tile([P, PAIR], U32, name="ctx_codes", align_bytes=64)
-                ctx_scales[pair] = work.tile([P, PAIR], U8, name="ctx_scales", align_bytes=64)
+                ctx_codes[pair] = work.tile([P, PAIR], U32, name="ctx_codes", align_bytes=64, bufs=3)
+                ctx_scales[pair] = work.tile([P, PAIR], U8, name="ctx_scales", align_bytes=64, bufs=3)
             points = slice(member * P, (member + 1) * P)
             nc.vector.quantize_mx(
                 out=ctx_codes[pair][:, points].bitcast(FP8X4),
@@ -238,7 +242,7 @@ def tile_i2p_crossattention_pa_kernel(tc, q, k, v, Wo_words, Wo_scales, bo, feat
             b, place = divmod(pair, POINTS // PAIR)
             points = slice(place * PAIR, (place + 1) * PAIR)
             bank = other_psum.tile([P, 2, PAIR], F32, name="y_bank", tag="other")
-            result = work.tile([P, 2, PAIR], F32, name="result")
+            result = work.tile([P, 2, PAIR], F32, name="result", bufs=4)
             for c in range(2):
                 o = 2 * part + c
                 nc.tensor.matmul_mx(
@@ -270,27 +274,30 @@ def tile_i2p_crossattention_pa_kernel(tc, q, k, v, Wo_words, Wo_scales, bo, feat
         for rows, transposed, chunk, copy in chunks[:HEAD_CHUNKS]:
             transpose_chunk(rows, transposed, chunk, copy)
 
-        for s in range(STEPS + PV_LAG + 2):
+        for s in range(STEPS + Y_LAG):
             transposing = 0 <= s - E_LAG < STEPS
             if s < STEPS:
                 energy(s, 0)
-            first = HEAD_CHUNKS + 2 * s
-            for rows, transposed, chunk, copy in chunks[first : first + 2]:
-                transpose_chunk(rows, transposed, chunk, copy)
+            if s >= 1:
+                first = HEAD_CHUNKS + 2 * (s - 1)
+                for rows, transposed, chunk, copy in chunks[first : first + 2]:
+                    transpose_chunk(rows, transposed, chunk, copy)
             if transposing:
                 transpose_e(s - E_LAG)
+            if 0 <= s - INV_LAG < STEPS:
+                transpose_inverse(s - INV_LAG)
             if s < STEPS:
                 energy(s, 1)
                 exponentials(s)
-            if 0 <= s + 1 - E_LAG < STEPS:
-                denominator(s + 1 - E_LAG)
+            if 1 <= s <= STEPS:
+                denominator(s - 1)
             if transposing:
                 quantise_e(s - E_LAG)
             b, i = divmod(s, POINT_TILES)
             if b < BATCH and 1 <= i <= PASSES:
                 quantise_v(b, i - 1)
-            if 0 <= s - PV_LAG - 2 < STEPS:
-                project((s - PV_LAG - 2) // 2, (s - PV_LAG - 2) % 2)
+            if 0 <= s - Y_LAG < STEPS:
+                project((s - Y_LAG) // 2, (s - Y_LAG) % 2)
             if 0 <= s - PV_LAG < STEPS:
                 attend(s - PV_LAG)
             if b < BATCH and i < PASSES:

@@ -27,7 +27,6 @@ CHUNK = 2 * P
 PAIR = 2 * P
 HEAD_CHUNKS = 5
 E_LAG = 2
-INV_LAG = 3
 PV_LAG = 4
 Y_LAG = 7
 FLOPS = 2 * BATCH * (2 * POINTS * POSITIONS * CHANNELS + POINTS * CHANNELS * CHANNELS)
@@ -40,7 +39,7 @@ def tile_i2p_crossattention_pa_kernel(tc, q, k, v, Wo_words, Wo_scales, bo, feat
         keep = ctx.enter_context(tc.tile_pool(name="keep", bufs=1))
         small = ctx.enter_context(tc.tile_pool(name="small", bufs=E_LAG + 1))
         work = ctx.enter_context(tc.tile_pool(name="work", bufs=2))
-        lagged = ctx.enter_context(tc.tile_pool(name="lagged", bufs=max(INV_LAG, PV_LAG - E_LAG) + 1))
+        lagged = ctx.enter_context(tc.tile_pool(name="lagged", bufs=PV_LAG))
         energy_psum = ctx.enter_context(tc.psum_pool(name="energy_psum", bufs=4))
         other_psum = ctx.enter_context(tc.psum_pool(name="other_psum", bufs=4))
 
@@ -207,7 +206,10 @@ def tile_i2p_crossattention_pa_kernel(tc, q, k, v, Wo_words, Wo_scales, bo, feat
 
         def attend(s):
             b = s // POINT_TILES
-            bank = other_psum.tile([P, PACK, P], F32, name="ctx_bank", tag="other")
+            if s + PV_LAG < STEPS:
+                bank = other_psum.tile([P, PACK, P], F32, name="ctx_bank", tag="other")
+            else:
+                bank = energy_psum.tile([P, PACK, P], F32, name="late_ctx_bank", tag="energy")
             for t in range(PACK):
                 channels = slice(t * P, (t + 1) * P)
                 for g in range(PASSES):
@@ -242,7 +244,7 @@ def tile_i2p_crossattention_pa_kernel(tc, q, k, v, Wo_words, Wo_scales, bo, feat
             b, place = divmod(pair, POINTS // PAIR)
             points = slice(place * PAIR, (place + 1) * PAIR)
             bank = other_psum.tile([P, 2, PAIR], F32, name="y_bank", tag="other")
-            result = work.tile([P, 2, PAIR], F32, name="result", bufs=4)
+            result = work.tile([P, 2, PAIR], F32, name="result", bufs=STEPS)
             for c in range(2):
                 o = 2 * part + c
                 nc.tensor.matmul_mx(
@@ -260,9 +262,7 @@ def tile_i2p_crossattention_pa_kernel(tc, q, k, v, Wo_words, Wo_scales, bo, feat
                     out=result[:, c, :], in0=bank[:, c, :], scalar=bias[:, o : o + 1], in1=feat[b][:, o, points],
                     op0=ALU.add, op1=ALU.add,
                 )
-            nc.sync.dma_start(
-                out=out[b].rearrange("(o p) n -> p o n", p=P)[:, 2 * part : 2 * part + 2, points], in_=result[:]
-            )
+                nc.sync.dma_start(out=out[b, o * P : (o + 1) * P, points], in_=result[:, c, :])
 
         chunks = []
         for b in range(BATCH):
@@ -284,8 +284,8 @@ def tile_i2p_crossattention_pa_kernel(tc, q, k, v, Wo_words, Wo_scales, bo, feat
                     transpose_chunk(rows, transposed, chunk, copy)
             if transposing:
                 transpose_e(s - E_LAG)
-            if 0 <= s - INV_LAG < STEPS:
-                transpose_inverse(s - INV_LAG)
+            if 0 <= s - PV_LAG < STEPS:
+                transpose_inverse(s - PV_LAG)
             if s < STEPS:
                 energy(s, 1)
                 exponentials(s)
@@ -296,9 +296,9 @@ def tile_i2p_crossattention_pa_kernel(tc, q, k, v, Wo_words, Wo_scales, bo, feat
             b, i = divmod(s, POINT_TILES)
             if b < BATCH and 1 <= i <= PASSES:
                 quantise_v(b, i - 1)
-            if 0 <= s - Y_LAG < STEPS:
-                project((s - Y_LAG) // 2, (s - Y_LAG) % 2)
             if 0 <= s - PV_LAG < STEPS:
                 attend(s - PV_LAG)
+            if 0 <= s - Y_LAG < STEPS:
+                project((s - Y_LAG) // 2, (s - Y_LAG) % 2)
             if b < BATCH and i < PASSES:
                 regroup_v(b, i)

@@ -108,6 +108,7 @@ def tile_i2p_crossattention_pa_kernel(tc, q, k, v, Wo_words, Wo_scales, bo, feat
 
         energy_banks, row_max, row_sums, e_rows, spread = {}, {}, {}, {}, {}
         e_grouped, e_codes, e_scales, inv_cols, v_grouped, ctx_codes, ctx_scales = {}, {}, {}, {}, {}, {}, {}
+        ctx_grouped = {}
 
         def transpose_chunk(rows, transposed, chunk, copy):
             bank = other_psum.tile([P, 2, CHUNK], F32, name="chunk_bank", tag="other")
@@ -222,13 +223,15 @@ def tile_i2p_crossattention_pa_kernel(tc, q, k, v, Wo_words, Wo_scales, bo, feat
                         start=(g == 0),
                         stop=(g == PASSES - 1),
                     )
-            grouped = work.tile([P, P, PACK], BF16, name="ctx_grouped", align_bytes=64)
+            ctx_grouped[s] = work.tile([P, P, PACK], BF16, name="ctx_grouped", align_bytes=64)
             nc.vector.tensor_tensor(
-                out=grouped[:],
+                out=ctx_grouped[s][:],
                 in0=bank[:].rearrange("p t n -> p n t"),
                 in1=inv_cols[s][:].unsqueeze(2).to_broadcast([P, P, PACK]),
                 op=ALU.mult,
             )
+
+        def quantise_ctx(s):
             pair, member = divmod(s, 2)
             if member == 0:
                 ctx_codes[pair] = work.tile([P, PAIR], U32, name="ctx_codes", align_bytes=64, bufs=3)
@@ -237,7 +240,7 @@ def tile_i2p_crossattention_pa_kernel(tc, q, k, v, Wo_words, Wo_scales, bo, feat
             nc.vector.quantize_mx(
                 out=ctx_codes[pair][:, points].bitcast(FP8X4),
                 scales=ctx_scales[pair][:, points],
-                in_=grouped[:].rearrange("p n t -> p (n t)"),
+                in_=ctx_grouped[s][:].rearrange("p n t -> p (n t)"),
             )
 
         def project(pair, part):
@@ -278,6 +281,8 @@ def tile_i2p_crossattention_pa_kernel(tc, q, k, v, Wo_words, Wo_scales, bo, feat
             transposing = 0 <= s - E_LAG < STEPS
             if s < STEPS:
                 energy(s, 0)
+            if 0 <= s - PV_LAG - 1 < STEPS:
+                quantise_ctx(s - PV_LAG - 1)
             if s >= 1:
                 first = HEAD_CHUNKS + 2 * (s - 1)
                 for rows, transposed, chunk, copy in chunks[first : first + 2]:

@@ -108,7 +108,7 @@ def tile_i2p_crossattention_pa_kernel(tc, q, k, v, Wo_words, Wo_scales, bo, feat
 
         energy_banks, row_max, row_sums, e_rows, spread = {}, {}, {}, {}, {}
         e_grouped, e_codes, e_scales, inv_cols, v_grouped, ctx_codes, ctx_scales = {}, {}, {}, {}, {}, {}, {}
-        ctx_grouped = {}
+        ctx_grouped, neg_maxima = {}, {}
 
         def transpose_chunk(rows, transposed, chunk, copy):
             bank = other_psum.tile([P, 2, CHUNK], F32, name="chunk_bank", tag="other")
@@ -137,12 +137,16 @@ def tile_i2p_crossattention_pa_kernel(tc, q, k, v, Wo_words, Wo_scales, bo, feat
             nc.vector.reduce_max(out=row_max[s][:, h : h + 1], in_=bank[:], axis=AXIS.X)
             energy_banks[(s, h)] = bank
 
-        def exponentials(s):
+        def negate_maximum(s):
             neg_max = small.tile([P, 1], F32, name="neg_max")
             nc.vector.tensor_scalar(
                 out=neg_max[:], in0=row_max[s][:, 0:1], scalar1=row_max[s][:, 1:2], scalar2=-1.0,
                 op0=ALU.max, op1=ALU.mult,
             )
+            neg_maxima[s] = neg_max
+
+        def exponentials(s):
+            neg_max = neg_maxima[s]
             e_rows[s] = lagged.tile([P, POSITIONS], BF16, name="e_rows")
             row_sums[s] = small.tile([P, HALVES], F32, name="row_sums")
             for h in range(HALVES):
@@ -153,7 +157,7 @@ def tile_i2p_crossattention_pa_kernel(tc, q, k, v, Wo_words, Wo_scales, bo, feat
 
         def denominator(s):
             scaled_sum = small.tile([P, 1], F32, name="scaled_sum")
-            nc.vector.tensor_scalar(
+            nc.gpsimd.tensor_scalar(
                 out=scaled_sum[:], in0=row_sums[s][:, 0:1], scalar1=row_sums[s][:, 1:2],
                 scalar2=math.sqrt(CHANNELS), op0=ALU.add, op1=ALU.mult,
             )
@@ -281,8 +285,6 @@ def tile_i2p_crossattention_pa_kernel(tc, q, k, v, Wo_words, Wo_scales, bo, feat
             transposing = 0 <= s - E_LAG < STEPS
             if s < STEPS:
                 energy(s, 0)
-            if 0 <= s - PV_LAG - 1 < STEPS:
-                quantise_ctx(s - PV_LAG - 1)
             if s >= 1:
                 first = HEAD_CHUNKS + 2 * (s - 1)
                 for rows, transposed, chunk, copy in chunks[first : first + 2]:
@@ -293,6 +295,10 @@ def tile_i2p_crossattention_pa_kernel(tc, q, k, v, Wo_words, Wo_scales, bo, feat
                 transpose_inverse(s - PV_LAG)
             if s < STEPS:
                 energy(s, 1)
+            if 0 <= s - PV_LAG - 1 < STEPS:
+                quantise_ctx(s - PV_LAG - 1)
+            if s < STEPS:
+                negate_maximum(s)
                 exponentials(s)
             if 1 <= s <= STEPS:
                 denominator(s - 1)

@@ -87,8 +87,8 @@ def tile_i2p_crossattention_pa_kernel(tc, q, k, v, Wo_words, Wo_scales, bo, feat
         def load_feat(b):
             nc.sync.dma_start(out=feat[b][:], in_=feat0[b].rearrange("(o p) n -> p o n", p=P))
 
-        nc.sync.dma_start(out=bias_rows[0:OUT_TILES, :], in_=bo.rearrange("(o p) -> o p", p=P))
         load_q_and_k(0)
+        nc.sync.dma_start(out=bias_rows[0:OUT_TILES, :], in_=bo.rearrange("(o p) -> o p", p=P))
         load_v(0)
         load_q_and_k(1)
         nc.sync.dma_start(out=w_codes[:].bitcast(I32), in_=Wo_words[0].rearrange("p n t -> p (n t)").bitcast(I32))
@@ -101,10 +101,10 @@ def tile_i2p_crossattention_pa_kernel(tc, q, k, v, Wo_words, Wo_scales, bo, feat
         load_v(1)
         load_feat(1)
 
-        nc.vector.tensor_copy(out=bias_rows_f32[:], in_=bias_rows[:])
-        bias_bank = other_psum.tile([P, P], F32, name="bias_bank", tag="other")
-        nc.tensor.transpose(bias_bank[:], bias_rows_f32[:], identity[:])
-        nc.vector.tensor_copy(out=bias[:], in_=bias_bank[:, 0:OUT_TILES])
+        def transpose_bias():
+            bias_bank = other_psum.tile([P, P], F32, name="bias_bank", tag="other")
+            nc.tensor.transpose(bias_bank[:], bias_rows_f32[:], identity[:])
+            nc.vector.tensor_copy(out=bias[:], in_=bias_bank[:, 0:OUT_TILES])
 
         energy_banks, row_max, row_sums, e_rows, spread = {}, {}, {}, {}, {}
         e_grouped, e_codes, e_scales, inv_cols, v_grouped, ctx_codes, ctx_scales = {}, {}, {}, {}, {}, {}, {}
@@ -281,6 +281,8 @@ def tile_i2p_crossattention_pa_kernel(tc, q, k, v, Wo_words, Wo_scales, bo, feat
         for rows, transposed, chunk, copy in chunks[:HEAD_CHUNKS]:
             transpose_chunk(rows, transposed, chunk, copy)
 
+        nc.vector.tensor_copy(out=bias_rows_f32[:], in_=bias_rows[:])
+
         for s in range(STEPS + Y_LAG):
             transposing = 0 <= s - E_LAG < STEPS
             if s < STEPS:
@@ -289,6 +291,8 @@ def tile_i2p_crossattention_pa_kernel(tc, q, k, v, Wo_words, Wo_scales, bo, feat
                 first = HEAD_CHUNKS + 2 * (s - 1)
                 for rows, transposed, chunk, copy in chunks[first : first + 2]:
                     transpose_chunk(rows, transposed, chunk, copy)
+            if s == 1:
+                transpose_bias()
             if transposing:
                 transpose_e(s - E_LAG)
             if 0 <= s - PV_LAG < STEPS:

@@ -44,6 +44,7 @@ def tile_i2p_crossattention_pa_kernel(tc, q, k, v, Wo_words, Wo_scales, bo, feat
         other_psum = ctx.enter_context(tc.psum_pool(name="other_psum", bufs=4))
 
         identity = keep.tile([P, P], F32, name="identity")
+        warm = keep.tile([P, BANK], BF16, name="warm")
         ones = keep.tile([P, P], F32, name="ones")
         bias_rows = keep.tile([P, P], BF16, name="bias_rows")
         bias_rows_f32 = keep.tile([P, P], F32, name="bias_rows_f32")
@@ -61,6 +62,7 @@ def tile_i2p_crossattention_pa_kernel(tc, q, k, v, Wo_words, Wo_scales, bo, feat
             v_codes.append(keep.tile([P, PASSES, CHANNELS], U32, name="v_codes%d" % b, align_bytes=64))
             v_scales.append(keep.tile([P, PASSES, CHANNELS], U8, name="v_scales%d" % b, align_bytes=64))
 
+        nc.vector.memset(warm[:], 0.0)
         nc.vector.memset(w_scales[:].bitcast(I32), 0)
         nc.vector.memset(bias_rows[:], 0.0)
         make_identity(nc, identity[:])
@@ -105,6 +107,14 @@ def tile_i2p_crossattention_pa_kernel(tc, q, k, v, Wo_words, Wo_scales, bo, feat
             bias_bank = other_psum.tile([P, P], F32, name="bias_bank", tag="other")
             nc.tensor.transpose(bias_bank[:], bias_rows_f32[:], identity[:])
             nc.vector.tensor_copy(out=bias[:], in_=bias_bank[:, 0:OUT_TILES])
+
+        warm_bank = energy_psum.tile([P, BANK], F32, name="warm_bank", tag="energy")
+
+        def warm_up(count):
+            for _ in range(count):
+                nc.tensor.matmul(warm_bank[:], lhsT=warm[:, 0:P], rhs=warm[:], start=True, stop=True)
+
+        warm_up(4)
 
         energy_banks, row_max, row_sums, e_rows, spread = {}, {}, {}, {}, {}
         e_grouped, e_codes, e_scales, inv_cols, v_grouped, ctx_codes, ctx_scales = {}, {}, {}, {}, {}, {}, {}

@@ -45,7 +45,6 @@ def tile_i2p_crossattention_pa_kernel(tc, q, k, v, Wo_words, Wo_scales, bo, feat
 
         identity = keep.tile([P, P], F32, name="identity")
         warm = keep.tile([P, BANK], BF16, name="warm")
-        ones = keep.tile([P, P], F32, name="ones")
         bias_rows = keep.tile([P, P], BF16, name="bias_rows")
         bias_rows_f32 = keep.tile([P, P], F32, name="bias_rows_f32")
         bias = keep.tile([P, OUT_TILES], F32, name="bias")
@@ -66,7 +65,6 @@ def tile_i2p_crossattention_pa_kernel(tc, q, k, v, Wo_words, Wo_scales, bo, feat
         nc.vector.memset(w_scales[:].bitcast(I32), 0)
         nc.vector.memset(bias_rows[:], 0.0)
         make_identity(nc, identity[:])
-        nc.gpsimd.memset(ones[:], 1.0)
 
         def load_chunk(rows, source, chunk):
             tiles = slice(2 * chunk, 2 * chunk + 2)
@@ -116,7 +114,7 @@ def tile_i2p_crossattention_pa_kernel(tc, q, k, v, Wo_words, Wo_scales, bo, feat
 
         warm_up(4)
 
-        energy_banks, row_max, row_sums, e_rows, spread = {}, {}, {}, {}, {}
+        energy_banks, row_max, row_sums, e_rows, inverses = {}, {}, {}, {}, {}
         e_grouped, e_codes, e_scales, inv_cols, v_grouped, ctx_codes, ctx_scales = {}, {}, {}, {}, {}, {}, {}
         ctx_grouped, neg_maxima = {}, {}
 
@@ -171,12 +169,8 @@ def tile_i2p_crossattention_pa_kernel(tc, q, k, v, Wo_words, Wo_scales, bo, feat
                 out=scaled_sum[:], in0=row_sums[s][:, 0:1], scalar1=row_sums[s][:, 1:2],
                 scalar2=math.sqrt(CHANNELS), op0=ALU.add, op1=ALU.mult,
             )
-            inverse = small.tile([P, 1], F32, name="inverse")
-            nc.vector.reciprocal(out=inverse[:], in_=scaled_sum[:])
-            spread[s] = lagged.tile([P, P], F32, name="spread")
-            nc.gpsimd.tensor_scalar(
-                out=spread[s][:], in0=ones[:], scalar1=inverse[:, 0:1], scalar2=0.0, op0=ALU.mult, op1=ALU.add
-            )
+            inverses[s] = lagged.tile([P, 1], F32, name="inverse")
+            nc.vector.reciprocal(out=inverses[s][:], in_=scaled_sum[:])
 
         def transpose_e(s):
             bank = other_psum.tile([P, PASSES, 2, P], F32, name="e_bank", tag="other")
@@ -192,7 +186,7 @@ def tile_i2p_crossattention_pa_kernel(tc, q, k, v, Wo_words, Wo_scales, bo, feat
 
         def transpose_inverse(s):
             inv_bank = other_psum.tile([P, P], F32, name="inv_bank", tag="other")
-            nc.tensor.transpose(inv_bank[:], spread[s][:], identity[:])
+            nc.tensor.transpose(inv_bank[:], inverses[s][:, 0:1].to_broadcast([P, P]), identity[:])
             inv_cols[s] = lagged.tile([P, P], F32, name="inv_cols")
             nc.scalar.copy(out=inv_cols[s][:], in_=inv_bank[:])
 

@@ -29,6 +29,7 @@ HEAD_CHUNKS = 5
 E_LAG = 2
 PV_LAG = 4
 Y_LAG = 7
+BY_POINTS = (6,)
 FLOPS = 2 * BATCH * (2 * POINTS * POSITIONS * CHANNELS + POINTS * CHANNELS * CHANNELS)
 
 
@@ -39,7 +40,7 @@ def tile_i2p_crossattention_pa_kernel(tc, q, k, v, Wo_words, Wo_scales, bo, feat
         keep = ctx.enter_context(tc.tile_pool(name="keep", bufs=1))
         small = ctx.enter_context(tc.tile_pool(name="small", bufs=E_LAG + 1))
         work = ctx.enter_context(tc.tile_pool(name="work", bufs=2))
-        lagged = ctx.enter_context(tc.tile_pool(name="lagged", bufs=PV_LAG))
+        lagged = ctx.enter_context(tc.tile_pool(name="lagged", bufs=STEPS))
         energy_psum = ctx.enter_context(tc.psum_pool(name="energy_psum", bufs=4))
         other_psum = ctx.enter_context(tc.psum_pool(name="other_psum", bufs=4))
 
@@ -66,15 +67,16 @@ def tile_i2p_crossattention_pa_kernel(tc, q, k, v, Wo_words, Wo_scales, bo, feat
         nc.vector.memset(bias_rows[:], 0.0)
         make_identity(nc, identity[:])
 
-        def load_chunk(rows, source, chunk):
-            tiles = slice(2 * chunk, 2 * chunk + 2)
+        def load_rows(rows, source, first, count):
+            tiles = slice(first, first + count)
             nc.sync.dma_start(out=rows[:, tiles, :], in_=source.rearrange("(a p) c -> p a c", p=P)[:, tiles, :])
 
         def load_q_and_k(b):
-            load_chunk(q_rows[b], q[b], 0)
+            load_rows(q_rows[b], q[b], 0, 1)
             for chunk in range(POSITIONS // CHUNK):
-                load_chunk(k_rows[b], k[b], chunk)
-            load_chunk(q_rows[b], q[b], 1)
+                load_rows(k_rows[b], k[b], 2 * chunk, 2)
+            load_rows(q_rows[b], q[b], 1, 1)
+            load_rows(q_rows[b], q[b], 2, 2)
 
         def load_v(b):
             for g in range(PASSES):
@@ -116,15 +118,18 @@ def tile_i2p_crossattention_pa_kernel(tc, q, k, v, Wo_words, Wo_scales, bo, feat
 
         energy_banks, row_max, row_sums, e_rows, inverses = {}, {}, {}, {}, {}
         e_grouped, e_codes, e_scales, inv_cols, v_grouped, ctx_codes, ctx_scales = {}, {}, {}, {}, {}, {}, {}
-        ctx_grouped, neg_maxima = {}, {}
+        ctx_grouped, neg_maxima, ctx_rows, e_banks, ctx_banks, y_banks = {}, {}, {}, {}, {}, {}
 
-        def transpose_chunk(rows, transposed, chunk, copy):
-            bank = other_psum.tile([P, 2, CHUNK], F32, name="chunk_bank", tag="other")
-            for a in range(2):
-                words = rows[:, 2 * chunk + a, :].bitcast(F32)
+        def transpose_rows(rows, transposed, tiles, copy, early=False):
+            if early:
+                bank = energy_psum.tile([P, 2, len(tiles) * P], F32, name="early_bank", tag="energy")
+            else:
+                bank = other_psum.tile([P, 2, len(tiles) * P], F32, name="rows_t_bank", tag="other")
+            for a, tile in enumerate(tiles):
+                words = rows[:, tile, :].bitcast(F32)
                 for w in range(2):
                     nc.tensor.transpose(bank[:, w, a * P : (a + 1) * P], words[:, w * P : (w + 1) * P], identity[:])
-            copy(out=transposed[:].bitcast(F32)[:, :, chunk * CHUNK : (chunk + 1) * CHUNK], in_=bank[:])
+            copy(out=transposed[:].bitcast(F32)[:, :, tiles[0] * P : (tiles[-1] + 1) * P], in_=bank[:])
 
         def energy(s, h):
             b, i = divmod(s, POINT_TILES)
@@ -140,10 +145,13 @@ def tile_i2p_crossattention_pa_kernel(tc, q, k, v, Wo_words, Wo_scales, bo, feat
                     start=(c == 0),
                     stop=(c == 3),
                 )
+            energy_banks[(s, h)] = bank
+
+        def maximum(s, h):
+            bank = energy_banks[(s, h)]
             if h == 0:
                 row_max[s] = small.tile([P, HALVES], F32, name="row_max")
             nc.vector.reduce_max(out=row_max[s][:, h : h + 1], in_=bank[:], axis=AXIS.X)
-            energy_banks[(s, h)] = bank
 
         def negate_maximum(s):
             neg_max = small.tile([P, 1], F32, name="neg_max")
@@ -178,6 +186,10 @@ def tile_i2p_crossattention_pa_kernel(tc, q, k, v, Wo_words, Wo_scales, bo, feat
             for c in range(2 * PASSES):
                 g, u = divmod(c, 2)
                 nc.tensor.transpose(bank[:, g, u, :], words[:, c * P : (c + 1) * P], identity[:])
+            e_banks[s] = bank
+
+        def copy_e(s):
+            bank = e_banks[s]
             e_grouped[s] = work.tile([P, PASSES, PACK * P], BF16, name="e_grouped", align_bytes=64)
             nc.scalar.copy(
                 out=e_grouped[s][:].bitcast(F32).rearrange("p g (n u) -> p g n u", u=2),
@@ -231,7 +243,11 @@ def tile_i2p_crossattention_pa_kernel(tc, q, k, v, Wo_words, Wo_scales, bo, feat
                         start=(g == 0),
                         stop=(g == PASSES - 1),
                     )
-            ctx_grouped[s] = work.tile([P, P, PACK], BF16, name="ctx_grouped", align_bytes=64)
+            ctx_banks[s] = bank
+
+        def divide_columns(s):
+            bank = ctx_banks[s]
+            ctx_grouped[s] = work.tile([P, P, PACK], BF16, name="ctx_grouped", align_bytes=64, bufs=4)
             nc.vector.tensor_tensor(
                 out=ctx_grouped[s][:],
                 in0=bank[:].rearrange("p t n -> p n t"),
@@ -239,9 +255,47 @@ def tile_i2p_crossattention_pa_kernel(tc, q, k, v, Wo_words, Wo_scales, bo, feat
                 op=ALU.mult,
             )
 
+        def attend_by_points(s):
+            b = s // POINT_TILES
+            bank = energy_psum.tile([P, CHANNELS], F32, name="rows_bank", tag="energy")
+            for g in range(PASSES):
+                nc.tensor.matmul_mx(
+                    out=bank[:],
+                    lhsT=e_codes[s][:, g, :].bitcast(FP8X4),
+                    lhsT_scale=e_scales[s][:, g, :],
+                    rhs=v_codes[b][:, g, :].bitcast(FP8X4),
+                    rhs_scale=v_scales[b][:, g, :],
+                    start=(g == 0),
+                    stop=(g == PASSES - 1),
+                )
+            ctx_banks[s] = bank
+
+        def divide_rows(s):
+            bank = ctx_banks[s]
+            ctx_rows[s] = work.tile([P, 2, P, 2], BF16, name="ctx_rows", bufs=6)
+            nc.scalar.activation(
+                out=ctx_rows[s][:], in_=bank[:].rearrange("n (u j i) -> n u i j", u=2, j=2), func=ACT.Copy,
+                scale=inverses[s][:, 0:1],
+            )
+
+        def transpose_ctx(s):
+            bank = other_psum.tile([P, 2, P], F32, name="ctx_t_bank", tag="other")
+            words = ctx_rows[s][:].rearrange("n u i j -> n (u i j)").bitcast(F32)
+            for u in range(2):
+                nc.tensor.transpose(bank[:, u, :], words[:, u * P : (u + 1) * P], identity[:])
+            ctx_banks[s] = bank
+
+        def copy_ctx(s):
+            bank = ctx_banks[s]
+            ctx_grouped[s] = work.tile([P, P, PACK], BF16, name="ctx_grouped", align_bytes=64, bufs=4)
+            nc.scalar.copy(
+                out=ctx_grouped[s][:].rearrange("p n t -> p (n t)").bitcast(F32).rearrange("p (n u) -> p n u", u=2),
+                in_=bank[:].rearrange("p u n -> p n u"),
+            )
+
         def quantise_ctx(s):
             pair, member = divmod(s, 2)
-            if member == 0:
+            if pair not in ctx_codes:
                 ctx_codes[pair] = work.tile([P, PAIR], U32, name="ctx_codes", align_bytes=64, bufs=3)
                 ctx_scales[pair] = work.tile([P, PAIR], U8, name="ctx_scales", align_bytes=64, bufs=3)
             points = slice(member * P, (member + 1) * P)
@@ -255,7 +309,6 @@ def tile_i2p_crossattention_pa_kernel(tc, q, k, v, Wo_words, Wo_scales, bo, feat
             b, place = divmod(pair, POINTS // PAIR)
             points = slice(place * PAIR, (place + 1) * PAIR)
             bank = other_psum.tile([P, 2, PAIR], F32, name="y_bank", tag="other")
-            result = work.tile([P, 2, PAIR], F32, name="result", bufs=STEPS)
             for c in range(2):
                 o = 2 * part + c
                 nc.tensor.matmul_mx(
@@ -267,6 +320,13 @@ def tile_i2p_crossattention_pa_kernel(tc, q, k, v, Wo_words, Wo_scales, bo, feat
                     start=True,
                     stop=True,
                 )
+            y_banks[(pair, part)] = bank
+
+        def add_and_store(pair, part):
+            b, place = divmod(pair, POINTS // PAIR)
+            points = slice(place * PAIR, (place + 1) * PAIR)
+            bank = y_banks[(pair, part)]
+            result = work.tile([P, 2, PAIR], F32, name="result", bufs=STEPS)
             for c in range(2):
                 o = 2 * part + c
                 nc.vector.scalar_tensor_tensor(
@@ -275,49 +335,77 @@ def tile_i2p_crossattention_pa_kernel(tc, q, k, v, Wo_words, Wo_scales, bo, feat
                 )
                 nc.sync.dma_start(out=out[b, o * P : (o + 1) * P, points], in_=result[:, c, :])
 
-        chunks = []
+        units = []
         for b in range(BATCH):
-            chunks.append((q_rows[b], q_t[b], 0, nc.scalar.copy))
+            units.append((q_rows[b], q_t[b], (0,)))
             for chunk in range(POSITIONS // CHUNK):
-                chunks.append((k_rows[b], k_t[b], chunk, nc.vector.tensor_copy if chunk % 2 == 0 else nc.scalar.copy))
-            chunks.append((q_rows[b], q_t[b], 1, nc.vector.tensor_copy))
-
-        for rows, transposed, chunk, copy in chunks[:HEAD_CHUNKS]:
-            transpose_chunk(rows, transposed, chunk, copy)
-
+                if b == 0:
+                    units.append((k_rows[b], k_t[b], (2 * chunk,)))
+                    units.append((k_rows[b], k_t[b], (2 * chunk + 1,)))
+                else:
+                    units.append((k_rows[b], k_t[b], (2 * chunk, 2 * chunk + 1)))
+            units.append((q_rows[b], q_t[b], (1,)))
+            units.append((q_rows[b], q_t[b], (2, 3)))
+        def unit(n, eng, early=False):
+            transpose_rows(*units[n], nc.vector.tensor_copy if eng == "v" else nc.scalar.copy, early)
+        for n in range(9):
+            unit(n, "sv"[n % 2], n in (1, 3, 5))
+        energy(0, 0)
+        unit(9, "s")
+        unit(10, "s")
+        maximum(0, 0)
+        regroup_v(0, 0)
+        energy(0, 1)
+        maximum(0, 1)
         nc.vector.tensor_copy(out=bias_rows_f32[:], in_=bias_rows[:])
-
-        for s in range(STEPS + Y_LAG):
-            transposing = 0 <= s - E_LAG < STEPS
-            if s < STEPS:
+        CH = {1: ((11, "v"),), 2: ((12, "v"), (13, "s")), 3: ((14, "v"), (15, "s"),(16, "v")), 4: ((17, "v"),)}
+        RV = {0: ((0, 1),), 3: ((1, 0),), 4: ((1, 1),)}
+        QV = {0: ((0, 0),), 1: ((0, 1),), 4: ((1, 0),), 5: ((1, 1),)}
+        PV = {k + PV_LAG: (k,) for k in range(8)}
+        YY = {k + Y_LAG: ((k // 2, k % 2),) for k in range(8)}
+        ET = {k + E_LAG: (k,) for k in range(8)}
+        QC = {k + PV_LAG + 1: (k,) for k in range(8)}
+        XT = {k + PV_LAG + 1: (k,) for k in BY_POINTS}
+        for s in range(16):
+            if 1 <= s < STEPS:
                 energy(s, 0)
-            if s >= 1:
-                first = HEAD_CHUNKS + 2 * (s - 1)
-                for rows, transposed, chunk, copy in chunks[first : first + 2]:
-                    transpose_chunk(rows, transposed, chunk, copy)
+                maximum(s, 0)
+            for n, eng in CH.get(s, ()):
+                unit(n, eng)
             if s == 1:
                 transpose_bias()
-            if transposing:
-                transpose_e(s - E_LAG)
-            if 0 <= s - PV_LAG < STEPS:
-                transpose_inverse(s - PV_LAG)
-            if s < STEPS:
+            for k in XT.get(s, ()):
+                transpose_ctx(k)
+                copy_ctx(k)
+            for k in ET.get(s, ()):
+                transpose_e(k)
+                copy_e(k)
+            for k in PV.get(s, ()):
+                if k not in BY_POINTS:
+                    transpose_inverse(k)
+            if 1 <= s < STEPS:
                 energy(s, 1)
-            if 0 <= s - PV_LAG - 1 < STEPS:
-                quantise_ctx(s - PV_LAG - 1)
+                maximum(s, 1)
+            for k in QC.get(s, ()):
+                quantise_ctx(k)
             if s < STEPS:
                 negate_maximum(s)
                 exponentials(s)
             if 1 <= s <= STEPS:
                 denominator(s - 1)
-            if transposing:
-                quantise_e(s - E_LAG)
-            b, i = divmod(s, POINT_TILES)
-            if b < BATCH and 1 <= i <= PASSES:
-                quantise_v(b, i - 1)
-            if 0 <= s - PV_LAG < STEPS:
-                attend(s - PV_LAG)
-            if 0 <= s - Y_LAG < STEPS:
-                project((s - Y_LAG) // 2, (s - Y_LAG) % 2)
-            if b < BATCH and i < PASSES:
-                regroup_v(b, i)
+            for k in ET.get(s, ()):
+                quantise_e(k)
+            for b, g in QV.get(s, ()):
+                quantise_v(b, g)
+            for k in PV.get(s, ()):
+                if k in BY_POINTS:
+                    attend_by_points(k)
+                    divide_rows(k)
+                else:
+                    attend(k)
+                    divide_columns(k)
+            for p, part in YY.get(s, ()):
+                project(p, part)
+                add_and_store(p, part)
+            for b, g in RV.get(s, ()):
+                regroup_v(b, g)

@@ -29,7 +29,7 @@ HEAD_CHUNKS = 5
 E_LAG = 2
 PV_LAG = 4
 Y_LAG = 7
-BY_POINTS = (6,)
+BY_POINTS = (5, 6)
 FLOPS = 2 * BATCH * (2 * POINTS * POSITIONS * CHANNELS + POINTS * CHANNELS * CHANNELS)
 
 
@@ -348,64 +348,161 @@ def tile_i2p_crossattention_pa_kernel(tc, q, k, v, Wo_words, Wo_scales, bo, feat
             units.append((q_rows[b], q_t[b], (2, 3)))
         def unit(n, eng, early=False):
             transpose_rows(*units[n], nc.vector.tensor_copy if eng == "v" else nc.scalar.copy, early)
-        for n in range(9):
-            unit(n, "sv"[n % 2], n in (1, 3, 5))
+        unit(0, 's', False)
+        unit(1, 'v', True)
+        unit(2, 's', False)
+        unit(3, 'v', True)
+        unit(4, 's', False)
+        unit(5, 'v', True)
+        unit(6, 's', False)
+        unit(7, 'v', False)
+        unit(8, 's', False)
         energy(0, 0)
-        unit(9, "s")
-        unit(10, "s")
+        unit(9, 's')
+        unit(10, 's')
         maximum(0, 0)
         regroup_v(0, 0)
         energy(0, 1)
         maximum(0, 1)
         nc.vector.tensor_copy(out=bias_rows_f32[:], in_=bias_rows[:])
-        CH = {1: ((11, "v"),), 2: ((12, "v"), (13, "s")), 3: ((14, "v"), (15, "s"),(16, "v")), 4: ((17, "v"),)}
-        RV = {0: ((0, 1),), 3: ((1, 0),), 4: ((1, 1),)}
-        QV = {0: ((0, 0),), 1: ((0, 1),), 4: ((1, 0),), 5: ((1, 1),)}
-        PV = {k + PV_LAG: (k,) for k in range(8)}
-        YY = {k + Y_LAG: ((k // 2, k % 2),) for k in range(8)}
-        ET = {k + E_LAG: (k,) for k in range(8)}
-        QC = {k + PV_LAG + 1: (k,) for k in range(8)}
-        XT = {k + PV_LAG + 1: (k,) for k in BY_POINTS}
-        for s in range(16):
-            if 1 <= s < STEPS:
-                energy(s, 0)
-                maximum(s, 0)
-            for n, eng in CH.get(s, ()):
-                unit(n, eng)
-            if s == 1:
-                transpose_bias()
-            for k in XT.get(s, ()):
-                transpose_ctx(k)
-                copy_ctx(k)
-            for k in ET.get(s, ()):
-                transpose_e(k)
-                copy_e(k)
-            for k in PV.get(s, ()):
-                if k not in BY_POINTS:
-                    transpose_inverse(k)
-            if 1 <= s < STEPS:
-                energy(s, 1)
-                maximum(s, 1)
-            for k in QC.get(s, ()):
-                quantise_ctx(k)
-            if s < STEPS:
-                negate_maximum(s)
-                exponentials(s)
-            if 1 <= s <= STEPS:
-                denominator(s - 1)
-            for k in ET.get(s, ()):
-                quantise_e(k)
-            for b, g in QV.get(s, ()):
-                quantise_v(b, g)
-            for k in PV.get(s, ()):
-                if k in BY_POINTS:
-                    attend_by_points(k)
-                    divide_rows(k)
-                else:
-                    attend(k)
-                    divide_columns(k)
-            for p, part in YY.get(s, ()):
-                project(p, part)
-                add_and_store(p, part)
-            for b, g in RV.get(s, ()):
-                regroup_v(b, g)
+        negate_maximum(0)
+        exponentials(0)
+        quantise_v(0, 0)
+        energy(1, 0)
+        maximum(1, 0)
+        unit(11, 's')
+        unit(12, 'v')
+        transpose_bias()
+        regroup_v(0, 1)
+        energy(1, 1)
+        maximum(1, 1)
+        negate_maximum(1)
+        exponentials(1)
+        denominator(0)
+        energy(2, 0)
+        maximum(2, 0)
+        unit(13, 's')
+        unit(14, 'v')
+        energy(2, 1)
+        maximum(2, 1)
+        negate_maximum(2)
+        exponentials(2)
+        denominator(1)
+        quantise_v(0, 1)
+        energy(3, 0)
+        maximum(3, 0)
+        unit(15, 's')
+        unit(16, 'v')
+        transpose_e(0)
+        copy_e(0)
+        regroup_v(1, 0)
+        energy(3, 1)
+        maximum(3, 1)
+        negate_maximum(3)
+        exponentials(3)
+        denominator(2)
+        quantise_e(0)
+        energy(4, 0)
+        maximum(4, 0)
+        unit(17, 'v')
+        transpose_e(1)
+        copy_e(1)
+        transpose_e(2)
+        copy_e(2)
+        regroup_v(1, 1)
+        energy(4, 1)
+        maximum(4, 1)
+        negate_maximum(4)
+        exponentials(4)
+        denominator(3)
+        quantise_e(1)
+        quantise_e(2)
+        quantise_v(1, 0)
+        energy(5, 0)
+        maximum(5, 0)
+        transpose_inverse(0)
+        transpose_inverse(1)
+        energy(5, 1)
+        maximum(5, 1)
+        negate_maximum(5)
+        exponentials(5)
+        denominator(4)
+        quantise_v(1, 1)
+        attend(0)
+        divide_columns(0)
+        attend(1)
+        divide_columns(1)
+        energy(6, 0)
+        maximum(6, 0)
+        transpose_e(3)
+        copy_e(3)
+        transpose_e(4)
+        copy_e(4)
+        energy(6, 1)
+        maximum(6, 1)
+        quantise_ctx(0)
+        quantise_ctx(1)
+        negate_maximum(6)
+        exponentials(6)
+        denominator(5)
+        quantise_e(3)
+        quantise_e(4)
+        energy(7, 0)
+        maximum(7, 0)
+        transpose_inverse(2)
+        transpose_inverse(3)
+        energy(7, 1)
+        transpose_e(5)
+        copy_e(5)
+        maximum(7, 1)
+        negate_maximum(7)
+        attend(2)
+        attend(3)
+        exponentials(7)
+        denominator(6)
+        divide_columns(2)
+        quantise_e(5)
+        divide_columns(3)
+        transpose_e(6)
+        copy_e(6)
+        transpose_inverse(4)
+        project(0, 0)
+        add_and_store(0, 0)
+        attend(4)
+        attend_by_points(5)
+        quantise_ctx(2)
+        quantise_ctx(3)
+        quantise_e(6)
+        divide_rows(5)
+        transpose_e(7)
+        copy_e(7)
+        divide_columns(4)
+        project(0, 1)
+        add_and_store(0, 1)
+        project(1, 0)
+        project(1, 1)
+        denominator(7)
+        quantise_ctx(4)
+        quantise_e(7)
+        add_and_store(1, 0)
+        transpose_ctx(5)
+        copy_ctx(5)
+        attend_by_points(6)
+        divide_rows(6)
+        transpose_inverse(7)
+        attend(7)
+        add_and_store(1, 1)
+        quantise_ctx(5)
+        divide_columns(7)
+        transpose_ctx(6)
+        copy_ctx(6)
+        project(2, 0)
+        project(2, 1)
+        quantise_ctx(6)
+        quantise_ctx(7)
+        add_and_store(2, 0)
+        project(3, 0)
+        project(3, 1)
+        add_and_store(2, 1)
+        add_and_store(3, 0)
+        add_and_store(3, 1)

@@ -227,7 +227,7 @@ def tile_i2p_crossattention_pa_kernel(tc, q, k, v, Wo_words, Wo_scales, bo, feat
 
         def attend(s):
             b = s // POINT_TILES
-            if s + PV_LAG < STEPS:
+            if s < 2:
                 bank = other_psum.tile([P, PACK, P], F32, name="ctx_bank", tag="other")
             else:
                 bank = energy_psum.tile([P, PACK, P], F32, name="late_ctx_bank", tag="energy")
@@ -451,45 +451,45 @@ def tile_i2p_crossattention_pa_kernel(tc, q, k, v, Wo_words, Wo_scales, bo, feat
         maximum(7, 0)
         transpose_inverse(2)
         transpose_inverse(3)
+        transpose_inverse(4)
         energy(7, 1)
         transpose_e(5)
         copy_e(5)
         maximum(7, 1)
         negate_maximum(7)
         attend(2)
-        attend(3)
         exponentials(7)
-        denominator(6)
-        divide_columns(2)
-        quantise_e(5)
-        divide_columns(3)
         transpose_e(6)
         copy_e(6)
-        transpose_inverse(4)
+        divide_columns(2)
+        quantise_e(5)
+        denominator(6)
+        attend(3)
         project(0, 0)
-        add_and_store(0, 0)
-        attend(4)
+        divide_columns(3)
         attend_by_points(5)
+        attend(4)
         quantise_ctx(2)
         quantise_ctx(3)
+        add_and_store(0, 0)
         quantise_e(6)
-        divide_rows(5)
+        denominator(7)
         transpose_e(7)
+        divide_rows(5)
         copy_e(7)
         divide_columns(4)
         project(0, 1)
-        add_and_store(0, 1)
+        attend_by_points(6)
         project(1, 0)
-        project(1, 1)
-        denominator(7)
+        add_and_store(0, 1)
+        divide_rows(6)
+        transpose_ctx(5)
+        transpose_inverse(7)
+        copy_ctx(5)
         quantise_ctx(4)
         quantise_e(7)
+        project(1, 1)
         add_and_store(1, 0)
-        transpose_ctx(5)
-        copy_ctx(5)
-        attend_by_points(6)
-        divide_rows(6)
-        transpose_inverse(7)
         attend(7)
         add_and_store(1, 1)
         quantise_ctx(5)

@@ -93,6 +93,7 @@ def tile_i2p_crossattention_pa_kernel(tc, q, k, v, Wo_words, Wo_scales, bo, feat
         nc.sync.dma_start(out=bias_rows[0:OUT_TILES, :], in_=bo.rearrange("(o p) -> o p", p=P))
         load_v(0)
         load_q_and_k(1)
+        load_v(1)
         nc.sync.dma_start(out=w_codes[:].bitcast(I32), in_=Wo_words[0].rearrange("p n t -> p (n t)").bitcast(I32))
         for quadrant in range(4):
             nc.sync.dma_start(
@@ -100,7 +101,6 @@ def tile_i2p_crossattention_pa_kernel(tc, q, k, v, Wo_words, Wo_scales, bo, feat
                 in_=Wo_scales[0, 4 * quadrant : 4 * quadrant + 4, :].bitcast(I32),
             )
         load_feat(0)
-        load_v(1)
         load_feat(1)
 
         def transpose_bias():
@@ -115,6 +115,9 @@ def tile_i2p_crossattention_pa_kernel(tc, q, k, v, Wo_words, Wo_scales, bo, feat
                 nc.tensor.matmul(warm_bank[:], lhsT=warm[:, 0:P], rhs=warm[:], start=True, stop=True)
 
         warm_up(4)
+
+        def keep_warm():
+            nc.tensor.matmul(warm_bank[:, 0:384], lhsT=warm[:, 0:P], rhs=warm[:, 0:384], start=True, stop=True)
 
         energy_banks, row_max, row_sums, e_rows, inverses = {}, {}, {}, {}, {}
         e_grouped, e_codes, e_scales, inv_cols, v_grouped, ctx_codes, ctx_scales = {}, {}, {}, {}, {}, {}, {}
@@ -349,12 +352,16 @@ def tile_i2p_crossattention_pa_kernel(tc, q, k, v, Wo_words, Wo_scales, bo, feat
         def unit(n, eng, early=False):
             transpose_rows(*units[n], nc.vector.tensor_copy if eng == "v" else nc.scalar.copy, early)
         unit(0, 's', False)
+        keep_warm()
         unit(1, 'v', True)
         unit(2, 's', False)
+        keep_warm()
         unit(3, 'v', True)
         unit(4, 's', False)
+        keep_warm()
         unit(5, 'v', True)
         unit(6, 's', False)
+        keep_warm()
         unit(7, 'v', False)
         unit(8, 's', False)
         energy(0, 0)

@@ -150,6 +150,23 @@ def tile_i2p_crossattention_pa_kernel(tc, q, k, v, Wo_words, Wo_scales, bo, feat
                 )
             energy_banks[(s, h)] = bank
 
+        def energy_columns(s, h, part):
+            b, i = divmod(s, POINT_TILES)
+            q_view = q_t[b][:].rearrange("p w (r j) -> p w r j", j=2)
+            k_view = k_t[b][:].rearrange("p w (r j) -> p w r j", j=2)
+            if part == 0:
+                energy_banks[(s, h)] = energy_psum.tile([P, BANK], F32, name="energy_bank", tag="energy")
+            first = h * BANK + part * CHUNK
+            for c in range(4):
+                w, j = divmod(c, 2)
+                nc.tensor.matmul(
+                    energy_banks[(s, h)][:, part * CHUNK : (part + 1) * CHUNK],
+                    lhsT=q_view[:, w, i * P : (i + 1) * P, j],
+                    rhs=k_view[:, w, first : first + CHUNK, j],
+                    start=(c == 0),
+                    stop=(c == 3),
+                )
+
         def maximum(s, h):
             bank = energy_banks[(s, h)]
             if h == 0:
@@ -361,15 +378,16 @@ def tile_i2p_crossattention_pa_kernel(tc, q, k, v, Wo_words, Wo_scales, bo, feat
         keep_warm()
         unit(5, 'v', True)
         unit(6, 's', False)
-        keep_warm()
+        energy_columns(0, 0, 0)
         unit(7, 'v', False)
         unit(8, 's', False)
-        energy(0, 0)
+        energy_columns(0, 0, 1)
         unit(9, 's')
         unit(10, 's')
+        energy_columns(0, 1, 0)
         maximum(0, 0)
         regroup_v(0, 0)
-        energy(0, 1)
+        energy_columns(0, 1, 1)
         maximum(0, 1)
         nc.vector.tensor_copy(out=bias_rows_f32[:], in_=bias_rows[:])
         negate_maximum(0)
@@ -378,7 +396,6 @@ def tile_i2p_crossattention_pa_kernel(tc, q, k, v, Wo_words, Wo_scales, bo, feat
         energy(1, 0)
         maximum(1, 0)
         unit(11, 's')
-        unit(12, 'v')
         transpose_bias()
         regroup_v(0, 1)
         energy(1, 1)
@@ -388,8 +405,8 @@ def tile_i2p_crossattention_pa_kernel(tc, q, k, v, Wo_words, Wo_scales, bo, feat
         denominator(0)
         energy(2, 0)
         maximum(2, 0)
+        unit(12, 'v')
         unit(13, 's')
-        unit(14, 'v')
         energy(2, 1)
         maximum(2, 1)
         negate_maximum(2)
@@ -398,6 +415,7 @@ def tile_i2p_crossattention_pa_kernel(tc, q, k, v, Wo_words, Wo_scales, bo, feat
         quantise_v(0, 1)
         energy(3, 0)
         maximum(3, 0)
+        unit(14, 'v')
         unit(15, 's')
         unit(16, 'v')
         transpose_e(0)

@@ -20,16 +20,13 @@ BANK = 512
 BATCH, POINTS, POSITIONS, CHANNELS = 2, 512, 1024, 512
 POINT_TILES = POINTS // P
 STEPS = BATCH * POINT_TILES
+LAST = STEPS - 1
 HALVES = POSITIONS // BANK
 PASSES = POSITIONS // (P * PACK)
 OUT_TILES = CHANNELS // P
-CHUNK = 2 * P
+POSITION_TILES = POSITIONS // P
 PAIR = 2 * P
-HEAD_CHUNKS = 5
-E_LAG = 2
-PV_LAG = 4
-Y_LAG = 7
-BY_POINTS = (5, 6)
+KEEP_WARM = 384
 FLOPS = 2 * BATCH * (2 * POINTS * POSITIONS * CHANNELS + POINTS * CHANNELS * CHANNELS)
 
 
@@ -38,7 +35,7 @@ def tile_i2p_crossattention_pa_kernel(tc, q, k, v, Wo_words, Wo_scales, bo, feat
     with ExitStack() as ctx:
         ctx.enter_context(tc.manual_schedule())
         keep = ctx.enter_context(tc.tile_pool(name="keep", bufs=1))
-        small = ctx.enter_context(tc.tile_pool(name="small", bufs=E_LAG + 1))
+        small = ctx.enter_context(tc.tile_pool(name="small", bufs=3))
         work = ctx.enter_context(tc.tile_pool(name="work", bufs=2))
         lagged = ctx.enter_context(tc.tile_pool(name="lagged", bufs=STEPS))
         energy_psum = ctx.enter_context(tc.psum_pool(name="energy_psum", bufs=4))
@@ -53,8 +50,8 @@ def tile_i2p_crossattention_pa_kernel(tc, q, k, v, Wo_words, Wo_scales, bo, feat
         w_scales = keep.tile([P, CHANNELS], U8, name="w_scales", align_bytes=64)
         q_rows, k_rows, v_rows, feat, q_t, k_t, v_codes, v_scales = [], [], [], [], [], [], [], []
         for b in range(BATCH):
-            q_rows.append(keep.tile([P, POINTS // P, CHANNELS], BF16, name="q_rows%d" % b))
-            k_rows.append(keep.tile([P, POSITIONS // P, CHANNELS], BF16, name="k_rows%d" % b))
+            q_rows.append(keep.tile([P, POINT_TILES, CHANNELS], BF16, name="q_rows%d" % b))
+            k_rows.append(keep.tile([P, POSITION_TILES, CHANNELS], BF16, name="k_rows%d" % b))
             feat.append(keep.tile([P, OUT_TILES, POINTS], BF16, name="feat%d" % b))
             v_rows.append(keep.tile([P, PASSES, PACK, CHANNELS], BF16, name="v_rows%d" % b))
             q_t.append(keep.tile([P, 2, 2 * POINTS], BF16, name="q_t%d" % b))
@@ -71,29 +68,31 @@ def tile_i2p_crossattention_pa_kernel(tc, q, k, v, Wo_words, Wo_scales, bo, feat
             tiles = slice(first, first + count)
             nc.sync.dma_start(out=rows[:, tiles, :], in_=source.rearrange("(a p) c -> p a c", p=P)[:, tiles, :])
 
-        def load_q_and_k(b):
+        def load_first_q_and_k(b):
             load_rows(q_rows[b], q[b], 0, 1)
-            for chunk in range(POSITIONS // CHUNK):
-                load_rows(k_rows[b], k[b], 2 * chunk, 2)
+            for tile in range(0, POSITION_TILES, 2):
+                load_rows(k_rows[b], k[b], tile, 2)
             load_rows(q_rows[b], q[b], 1, 1)
-            load_rows(q_rows[b], q[b], 2, 2)
 
-        def load_v(b):
-            for g in range(PASSES):
-                positions = slice(g * P * PACK, (g + 1) * P * PACK)
-                nc.sync.dma_start(
-                    out=v_rows[b][:, g].rearrange("p (u j) c -> p u (j c)", j=2),
-                    in_=v[b, positions, :].rearrange("(u p j) c -> p u (j c)", u=2, j=2),
-                )
+        def load_v(b, g):
+            positions = slice(g * P * PACK, (g + 1) * P * PACK)
+            nc.sync.dma_start(
+                out=v_rows[b][:, g].rearrange("p (u j) c -> p u (j c)", j=2),
+                in_=v[b, positions, :].rearrange("(u p j) c -> p u (j c)", u=2, j=2),
+            )
 
         def load_feat(b):
             nc.sync.dma_start(out=feat[b][:], in_=feat0[b].rearrange("(o p) n -> p o n", p=P))
 
-        load_q_and_k(0)
+        load_first_q_and_k(0)
+        load_v(0, 0)
+        load_rows(q_rows[0], q[0], 2, 2)
         nc.sync.dma_start(out=bias_rows[0:OUT_TILES, :], in_=bo.rearrange("(o p) -> o p", p=P))
-        load_v(0)
-        load_q_and_k(1)
-        load_v(1)
+        load_v(0, 1)
+        load_first_q_and_k(1)
+        load_rows(q_rows[1], q[1], 2, 2)
+        load_v(1, 0)
+        load_v(1, 1)
         nc.sync.dma_start(out=w_codes[:].bitcast(I32), in_=Wo_words[0].rearrange("p n t -> p (n t)").bitcast(I32))
         for quadrant in range(4):
             nc.sync.dma_start(
@@ -103,92 +102,70 @@ def tile_i2p_crossattention_pa_kernel(tc, q, k, v, Wo_words, Wo_scales, bo, feat
         load_feat(0)
         load_feat(1)
 
-        def transpose_bias():
-            bias_bank = other_psum.tile([P, P], F32, name="bias_bank", tag="other")
-            nc.tensor.transpose(bias_bank[:], bias_rows_f32[:], identity[:])
-            nc.vector.tensor_copy(out=bias[:], in_=bias_bank[:, 0:OUT_TILES])
-
         warm_bank = energy_psum.tile([P, BANK], F32, name="warm_bank", tag="energy")
 
-        def warm_up(count):
-            for _ in range(count):
-                nc.tensor.matmul(warm_bank[:], lhsT=warm[:, 0:P], rhs=warm[:], start=True, stop=True)
+        def multiply_zeros(columns):
+            nc.tensor.matmul(warm_bank[:, 0:columns], lhsT=warm[:, 0:P], rhs=warm[:, 0:columns], start=True, stop=True)
 
-        warm_up(4)
+        energy_banks, row_max, neg_maxima, row_sums, inverses = {}, {}, {}, {}, {}
+        e_rows, e_banks, e_grouped, e_codes, e_scales, v_grouped = {}, {}, {}, {}, {}, {}
+        inv_cols, ctx_banks, ctx_rows, ctx_grouped, ctx_codes, ctx_scales, y_banks = {}, {}, {}, {}, {}, {}, {}
 
-        def keep_warm():
-            nc.tensor.matmul(warm_bank[:, 0:384], lhsT=warm[:, 0:P], rhs=warm[:, 0:384], start=True, stop=True)
+        def transpose_bias():
+            bank = other_psum.tile([P, P], F32, name="bias_bank", tag="other")
+            nc.tensor.transpose(bank[:], bias_rows_f32[:], identity[:])
+            nc.vector.tensor_copy(out=bias[:], in_=bank[:, 0:OUT_TILES])
 
-        energy_banks, row_max, row_sums, e_rows, inverses = {}, {}, {}, {}, {}
-        e_grouped, e_codes, e_scales, inv_cols, v_grouped, ctx_codes, ctx_scales = {}, {}, {}, {}, {}, {}, {}
-        ctx_grouped, neg_maxima, ctx_rows, e_banks, ctx_banks, y_banks = {}, {}, {}, {}, {}, {}
-
-        def transpose_rows(rows, transposed, tiles, copy, early=False):
-            if early:
-                bank = energy_psum.tile([P, 2, len(tiles) * P], F32, name="early_bank", tag="energy")
-            else:
-                bank = other_psum.tile([P, 2, len(tiles) * P], F32, name="rows_t_bank", tag="other")
-            for a, tile in enumerate(tiles):
-                words = rows[:, tile, :].bitcast(F32)
+        def transpose_rows(rows, transposed, first, count, copy, pool):
+            tag = "energy" if pool is energy_psum else "other"
+            bank = pool.tile([P, 2, count * P], F32, name="rows_bank", tag=tag)
+            for a in range(count):
+                words = rows[:, first + a, :].bitcast(F32)
                 for w in range(2):
                     nc.tensor.transpose(bank[:, w, a * P : (a + 1) * P], words[:, w * P : (w + 1) * P], identity[:])
-            copy(out=transposed[:].bitcast(F32)[:, :, tiles[0] * P : (tiles[-1] + 1) * P], in_=bank[:])
+            copy(out=transposed[:].bitcast(F32)[:, :, first * P : (first + count) * P], in_=bank[:])
 
-        def energy(s, h):
+        def transpose_q(b, first, count, copy):
+            transpose_rows(q_rows[b], q_t[b], first, count, copy, other_psum)
+
+        def transpose_k(b, first, count, copy, pool):
+            transpose_rows(k_rows[b], k_t[b], first, count, copy, pool)
+
+        def energy(s, h, start, stop):
             b, i = divmod(s, POINT_TILES)
             q_view = q_t[b][:].rearrange("p w (r j) -> p w r j", j=2)
             k_view = k_t[b][:].rearrange("p w (r j) -> p w r j", j=2)
-            bank = energy_psum.tile([P, BANK], F32, name="energy_bank", tag="energy")
-            for c in range(4):
-                w, j = divmod(c, 2)
-                nc.tensor.matmul(
-                    bank[:],
-                    lhsT=q_view[:, w, i * P : (i + 1) * P, j],
-                    rhs=k_view[:, w, h * BANK : (h + 1) * BANK, j],
-                    start=(c == 0),
-                    stop=(c == 3),
-                )
-            energy_banks[(s, h)] = bank
-
-        def energy_columns(s, h, part):
-            b, i = divmod(s, POINT_TILES)
-            q_view = q_t[b][:].rearrange("p w (r j) -> p w r j", j=2)
-            k_view = k_t[b][:].rearrange("p w (r j) -> p w r j", j=2)
-            if part == 0:
+            if start == 0:
                 energy_banks[(s, h)] = energy_psum.tile([P, BANK], F32, name="energy_bank", tag="energy")
-            first = h * BANK + part * CHUNK
             for c in range(4):
                 w, j = divmod(c, 2)
                 nc.tensor.matmul(
-                    energy_banks[(s, h)][:, part * CHUNK : (part + 1) * CHUNK],
+                    energy_banks[(s, h)][:, start:stop],
                     lhsT=q_view[:, w, i * P : (i + 1) * P, j],
-                    rhs=k_view[:, w, first : first + CHUNK, j],
+                    rhs=k_view[:, w, h * BANK + start : h * BANK + stop, j],
                     start=(c == 0),
                     stop=(c == 3),
                 )
 
         def maximum(s, h):
-            bank = energy_banks[(s, h)]
             if h == 0:
                 row_max[s] = small.tile([P, HALVES], F32, name="row_max")
-            nc.vector.reduce_max(out=row_max[s][:, h : h + 1], in_=bank[:], axis=AXIS.X)
+            nc.vector.reduce_max(out=row_max[s][:, h : h + 1], in_=energy_banks[(s, h)][:], axis=AXIS.X)
 
         def negate_maximum(s):
-            neg_max = small.tile([P, 1], F32, name="neg_max")
+            neg_maxima[s] = small.tile([P, 1], F32, name="neg_max")
             nc.vector.tensor_scalar(
-                out=neg_max[:], in0=row_max[s][:, 0:1], scalar1=row_max[s][:, 1:2], scalar2=-1.0,
+                out=neg_maxima[s][:], in0=row_max[s][:, 0:1], scalar1=row_max[s][:, 1:2], scalar2=-1.0,
                 op0=ALU.max, op1=ALU.mult,
             )
-            neg_maxima[s] = neg_max
 
         def exponentials(s):
-            neg_max = neg_maxima[s]
             e_rows[s] = lagged.tile([P, POSITIONS], BF16, name="e_rows")
             row_sums[s] = small.tile([P, HALVES], F32, name="row_sums")
             for h in range(HALVES):
                 nc.scalar.activation(
                     out=e_rows[s][:, h * BANK : (h + 1) * BANK], in_=energy_banks[(s, h)][:], func=ACT.Exp,
-                    bias=neg_max[:], scale=1.0, accum_out=row_sums[s][:, h : h + 1],
+                    bias=neg_maxima[s][:], scale=1.0, accum_out=row_sums[s][:, h : h + 1],
                 )
 
         def denominator(s):
@@ -200,27 +177,25 @@ def tile_i2p_crossattention_pa_kernel(tc, q, k, v, Wo_words, Wo_scales, bo, feat
             inverses[s] = lagged.tile([P, 1], F32, name="inverse")
             nc.vector.reciprocal(out=inverses[s][:], in_=scaled_sum[:])
 
+        def transpose_inverse(s):
+            bank = other_psum.tile([P, P], F32, name="inv_bank", tag="other")
+            nc.tensor.transpose(bank[:], inverses[s][:, 0:1].to_broadcast([P, P]), identity[:])
+            inv_cols[s] = lagged.tile([P, P], F32, name="inv_cols")
+            nc.scalar.copy(out=inv_cols[s][:], in_=bank[:])
+
         def transpose_e(s):
-            bank = other_psum.tile([P, PASSES, 2, P], F32, name="e_bank", tag="other")
+            e_banks[s] = other_psum.tile([P, PASSES, 2, P], F32, name="e_bank", tag="other")
             words = e_rows[s][:].bitcast(F32)
             for c in range(2 * PASSES):
                 g, u = divmod(c, 2)
-                nc.tensor.transpose(bank[:, g, u, :], words[:, c * P : (c + 1) * P], identity[:])
-            e_banks[s] = bank
+                nc.tensor.transpose(e_banks[s][:, g, u, :], words[:, c * P : (c + 1) * P], identity[:])
 
         def copy_e(s):
-            bank = e_banks[s]
             e_grouped[s] = work.tile([P, PASSES, PACK * P], BF16, name="e_grouped", align_bytes=64)
             nc.scalar.copy(
                 out=e_grouped[s][:].bitcast(F32).rearrange("p g (n u) -> p g n u", u=2),
-                in_=bank[:].rearrange("p g u n -> p g n u"),
+                in_=e_banks[s][:].rearrange("p g u n -> p g n u"),
             )
-
-        def transpose_inverse(s):
-            inv_bank = other_psum.tile([P, P], F32, name="inv_bank", tag="other")
-            nc.tensor.transpose(inv_bank[:], inverses[s][:, 0:1].to_broadcast([P, P]), identity[:])
-            inv_cols[s] = lagged.tile([P, P], F32, name="inv_cols")
-            nc.scalar.copy(out=inv_cols[s][:], in_=inv_bank[:])
 
         def quantise_e(s):
             e_codes[s] = lagged.tile([P, PASSES, P], U32, name="e_codes", align_bytes=64)
@@ -245,17 +220,15 @@ def tile_i2p_crossattention_pa_kernel(tc, q, k, v, Wo_words, Wo_scales, bo, feat
                 in_=v_grouped[(b, g)][:].rearrange("p t i row -> p (t i row)"),
             )
 
-        def attend(s):
+        def attend(s, pool):
             b = s // POINT_TILES
-            if s < 2:
-                bank = other_psum.tile([P, PACK, P], F32, name="ctx_bank", tag="other")
-            else:
-                bank = energy_psum.tile([P, PACK, P], F32, name="late_ctx_bank", tag="energy")
+            tag = "energy" if pool is energy_psum else "other"
+            ctx_banks[s] = pool.tile([P, PACK, P], F32, name="ctx_bank", tag=tag)
             for t in range(PACK):
                 channels = slice(t * P, (t + 1) * P)
                 for g in range(PASSES):
                     nc.tensor.matmul_mx(
-                        out=bank[:, t, :],
+                        out=ctx_banks[s][:, t, :],
                         lhsT=v_codes[b][:, g, channels].bitcast(FP8X4),
                         lhsT_scale=v_scales[b][:, g, channels],
                         rhs=e_codes[s][:, g, :].bitcast(FP8X4),
@@ -263,24 +236,22 @@ def tile_i2p_crossattention_pa_kernel(tc, q, k, v, Wo_words, Wo_scales, bo, feat
                         start=(g == 0),
                         stop=(g == PASSES - 1),
                     )
-            ctx_banks[s] = bank
 
-        def divide_columns(s):
-            bank = ctx_banks[s]
-            ctx_grouped[s] = work.tile([P, P, PACK], BF16, name="ctx_grouped", align_bytes=64, bufs=4)
+        def divide(s):
+            ctx_grouped[s] = lagged.tile([P, P, PACK], BF16, name="ctx_grouped", align_bytes=64)
             nc.vector.tensor_tensor(
                 out=ctx_grouped[s][:],
-                in0=bank[:].rearrange("p t n -> p n t"),
+                in0=ctx_banks[s][:].rearrange("p t n -> p n t"),
                 in1=inv_cols[s][:].unsqueeze(2).to_broadcast([P, P, PACK]),
                 op=ALU.mult,
             )
 
         def attend_by_points(s):
             b = s // POINT_TILES
-            bank = energy_psum.tile([P, CHANNELS], F32, name="rows_bank", tag="energy")
+            ctx_banks[s] = energy_psum.tile([P, CHANNELS], F32, name="ctx_rows_bank", tag="energy")
             for g in range(PASSES):
                 nc.tensor.matmul_mx(
-                    out=bank[:],
+                    out=ctx_banks[s][:],
                     lhsT=e_codes[s][:, g, :].bitcast(FP8X4),
                     lhsT_scale=e_scales[s][:, g, :],
                     rhs=v_codes[b][:, g, :].bitcast(FP8X4),
@@ -288,36 +259,32 @@ def tile_i2p_crossattention_pa_kernel(tc, q, k, v, Wo_words, Wo_scales, bo, feat
                     start=(g == 0),
                     stop=(g == PASSES - 1),
                 )
-            ctx_banks[s] = bank
 
-        def divide_rows(s):
-            bank = ctx_banks[s]
-            ctx_rows[s] = work.tile([P, 2, P, 2], BF16, name="ctx_rows", bufs=6)
+        def divide_by_points(s):
+            ctx_rows[s] = work.tile([P, 2, P, 2], BF16, name="ctx_rows")
             nc.scalar.activation(
-                out=ctx_rows[s][:], in_=bank[:].rearrange("n (u j i) -> n u i j", u=2, j=2), func=ACT.Copy,
+                out=ctx_rows[s][:], in_=ctx_banks[s][:].rearrange("n (u j i) -> n u i j", u=2, j=2), func=ACT.Copy,
                 scale=inverses[s][:, 0:1],
             )
 
         def transpose_ctx(s):
-            bank = other_psum.tile([P, 2, P], F32, name="ctx_t_bank", tag="other")
+            ctx_banks[s] = other_psum.tile([P, 2, P], F32, name="ctx_t_bank", tag="other")
             words = ctx_rows[s][:].rearrange("n u i j -> n (u i j)").bitcast(F32)
             for u in range(2):
-                nc.tensor.transpose(bank[:, u, :], words[:, u * P : (u + 1) * P], identity[:])
-            ctx_banks[s] = bank
+                nc.tensor.transpose(ctx_banks[s][:, u, :], words[:, u * P : (u + 1) * P], identity[:])
 
         def copy_ctx(s):
-            bank = ctx_banks[s]
-            ctx_grouped[s] = work.tile([P, P, PACK], BF16, name="ctx_grouped", align_bytes=64, bufs=4)
+            ctx_grouped[s] = lagged.tile([P, P, PACK], BF16, name="ctx_grouped", align_bytes=64)
             nc.scalar.copy(
                 out=ctx_grouped[s][:].rearrange("p n t -> p (n t)").bitcast(F32).rearrange("p (n u) -> p n u", u=2),
-                in_=bank[:].rearrange("p u n -> p n u"),
+                in_=ctx_banks[s][:].rearrange("p u n -> p n u"),
             )
 
         def quantise_ctx(s):
             pair, member = divmod(s, 2)
-            if pair not in ctx_codes:
-                ctx_codes[pair] = work.tile([P, PAIR], U32, name="ctx_codes", align_bytes=64, bufs=3)
-                ctx_scales[pair] = work.tile([P, PAIR], U8, name="ctx_scales", align_bytes=64, bufs=3)
+            if member == 0:
+                ctx_codes[pair] = lagged.tile([P, PAIR], U32, name="ctx_codes", align_bytes=64)
+                ctx_scales[pair] = lagged.tile([P, PAIR], U8, name="ctx_scales", align_bytes=64)
             points = slice(member * P, (member + 1) * P)
             nc.vector.quantize_mx(
                 out=ctx_codes[pair][:, points].bitcast(FP8X4),
@@ -326,13 +293,11 @@ def tile_i2p_crossattention_pa_kernel(tc, q, k, v, Wo_words, Wo_scales, bo, feat
             )
 
         def project(pair, part):
-            b, place = divmod(pair, POINTS // PAIR)
-            points = slice(place * PAIR, (place + 1) * PAIR)
-            bank = other_psum.tile([P, 2, PAIR], F32, name="y_bank", tag="other")
+            y_banks[(pair, part)] = other_psum.tile([P, 2, PAIR], F32, name="y_bank", tag="other")
             for c in range(2):
                 o = 2 * part + c
                 nc.tensor.matmul_mx(
-                    out=bank[:, c, :],
+                    out=y_banks[(pair, part)][:, c, :],
                     lhsT=w_codes[:, o * P : (o + 1) * P].bitcast(FP8X4),
                     lhsT_scale=w_scales[:, o * P : (o + 1) * P],
                     rhs=ctx_codes[pair][:].bitcast(FP8X4),
@@ -340,191 +305,145 @@ def tile_i2p_crossattention_pa_kernel(tc, q, k, v, Wo_words, Wo_scales, bo, feat
                     start=True,
                     stop=True,
                 )
-            y_banks[(pair, part)] = bank
 
         def add_and_store(pair, part):
             b, place = divmod(pair, POINTS // PAIR)
             points = slice(place * PAIR, (place + 1) * PAIR)
-            bank = y_banks[(pair, part)]
-            result = work.tile([P, 2, PAIR], F32, name="result", bufs=STEPS)
+            result = lagged.tile([P, 2, PAIR], F32, name="result")
             for c in range(2):
                 o = 2 * part + c
                 nc.vector.scalar_tensor_tensor(
-                    out=result[:, c, :], in0=bank[:, c, :], scalar=bias[:, o : o + 1], in1=feat[b][:, o, points],
-                    op0=ALU.add, op1=ALU.add,
+                    out=result[:, c, :], in0=y_banks[(pair, part)][:, c, :], scalar=bias[:, o : o + 1],
+                    in1=feat[b][:, o, points], op0=ALU.add, op1=ALU.add,
                 )
                 nc.sync.dma_start(out=out[b, o * P : (o + 1) * P, points], in_=result[:, c, :])
 
-        units = []
-        for b in range(BATCH):
-            units.append((q_rows[b], q_t[b], (0,)))
-            for chunk in range(POSITIONS // CHUNK):
-                if b == 0:
-                    units.append((k_rows[b], k_t[b], (2 * chunk,)))
-                    units.append((k_rows[b], k_t[b], (2 * chunk + 1,)))
-                else:
-                    units.append((k_rows[b], k_t[b], (2 * chunk, 2 * chunk + 1)))
-            units.append((q_rows[b], q_t[b], (1,)))
-            units.append((q_rows[b], q_t[b], (2, 3)))
-        def unit(n, eng, early=False):
-            transpose_rows(*units[n], nc.vector.tensor_copy if eng == "v" else nc.scalar.copy, early)
-        unit(0, 's', False)
-        keep_warm()
-        unit(1, 'v', True)
-        unit(2, 's', False)
-        keep_warm()
-        unit(3, 'v', True)
-        unit(4, 's', False)
-        keep_warm()
-        unit(5, 'v', True)
-        unit(6, 's', False)
-        energy_columns(0, 0, 0)
-        unit(7, 'v', False)
-        unit(8, 's', False)
-        energy_columns(0, 0, 1)
-        unit(9, 's')
-        unit(10, 's')
-        energy_columns(0, 1, 0)
+        scalar_copy, vector_copy = nc.scalar.copy, nc.vector.tensor_copy
+
+        for count in range(4):
+            multiply_zeros(BANK)
+        transpose_q(0, 0, 1, scalar_copy)
+        multiply_zeros(KEEP_WARM)
+        for tile in range(POSITION_TILES):
+            transpose_k(
+                0, tile, 1, vector_copy if tile % 2 == 0 else scalar_copy, energy_psum if tile in (0, 2) else other_psum
+            )
+            if tile in (1, 3):
+                multiply_zeros(KEEP_WARM)
+            if tile == 5:
+                energy(0, 0, 0, PAIR)
+            if tile == 7:
+                energy(0, 0, PAIR, BANK)
+        transpose_q(0, 1, 1, scalar_copy)
+        energy(0, 1, 0, PAIR)
         maximum(0, 0)
         regroup_v(0, 0)
-        energy_columns(0, 1, 1)
+        energy(0, 1, PAIR, BANK)
+        transpose_q(0, 2, 2, scalar_copy)
         maximum(0, 1)
         nc.vector.tensor_copy(out=bias_rows_f32[:], in_=bias_rows[:])
         negate_maximum(0)
         exponentials(0)
         quantise_v(0, 0)
-        energy(1, 0)
-        maximum(1, 0)
-        unit(11, 's')
-        transpose_bias()
-        regroup_v(0, 1)
-        energy(1, 1)
-        maximum(1, 1)
-        negate_maximum(1)
-        exponentials(1)
-        denominator(0)
-        energy(2, 0)
-        maximum(2, 0)
-        unit(12, 'v')
-        unit(13, 's')
-        energy(2, 1)
-        maximum(2, 1)
-        negate_maximum(2)
-        exponentials(2)
-        denominator(1)
-        quantise_v(0, 1)
-        energy(3, 0)
-        maximum(3, 0)
-        unit(14, 'v')
-        unit(15, 's')
-        unit(16, 'v')
-        transpose_e(0)
-        copy_e(0)
-        regroup_v(1, 0)
-        energy(3, 1)
-        maximum(3, 1)
-        negate_maximum(3)
-        exponentials(3)
-        denominator(2)
-        quantise_e(0)
-        energy(4, 0)
-        maximum(4, 0)
-        unit(17, 'v')
-        transpose_e(1)
-        copy_e(1)
-        transpose_e(2)
-        copy_e(2)
-        regroup_v(1, 1)
-        energy(4, 1)
-        maximum(4, 1)
-        negate_maximum(4)
-        exponentials(4)
-        denominator(3)
-        quantise_e(1)
-        quantise_e(2)
-        quantise_v(1, 0)
-        energy(5, 0)
-        maximum(5, 0)
-        transpose_inverse(0)
-        transpose_inverse(1)
-        energy(5, 1)
-        maximum(5, 1)
-        negate_maximum(5)
-        exponentials(5)
-        denominator(4)
-        quantise_v(1, 1)
-        attend(0)
-        divide_columns(0)
-        attend(1)
-        divide_columns(1)
-        energy(6, 0)
-        maximum(6, 0)
-        transpose_e(3)
-        copy_e(3)
-        transpose_e(4)
-        copy_e(4)
-        energy(6, 1)
-        maximum(6, 1)
-        quantise_ctx(0)
-        quantise_ctx(1)
-        negate_maximum(6)
-        exponentials(6)
-        denominator(5)
-        quantise_e(3)
-        quantise_e(4)
-        energy(7, 0)
-        maximum(7, 0)
-        transpose_inverse(2)
-        transpose_inverse(3)
-        transpose_inverse(4)
-        energy(7, 1)
+
+        for s in range(1, LAST):
+            ready = (0,) if s == 3 else (s - 3, s - 2) if s in (4, 6) else ()
+            energy(s, 0, 0, BANK)
+            maximum(s, 0)
+            if s == 1:
+                transpose_bias()
+            if s == 2:
+                transpose_q(1, 0, 1, scalar_copy)
+                transpose_k(1, 0, 2, vector_copy, other_psum)
+                transpose_k(1, 2, 2, scalar_copy, other_psum)
+            if s == 3:
+                transpose_k(1, 4, 2, vector_copy, other_psum)
+                transpose_k(1, 6, 2, scalar_copy, other_psum)
+                transpose_q(1, 1, 1, vector_copy)
+            if s == 4:
+                transpose_q(1, 2, 2, vector_copy)
+            for r in ready:
+                transpose_e(r)
+                copy_e(r)
+            if s == 5:
+                transpose_inverse(0)
+                transpose_inverse(1)
+            if s == 1:
+                regroup_v(0, 1)
+            if s in (3, 4):
+                regroup_v(1, s - 3)
+            energy(s, 1, 0, BANK)
+            maximum(s, 1)
+            if s == 6:
+                quantise_ctx(0)
+                quantise_ctx(1)
+            negate_maximum(s)
+            exponentials(s)
+            denominator(s - 1)
+            for r in ready:
+                quantise_e(r)
+            if s == 2:
+                quantise_v(0, 1)
+            if s in (4, 5):
+                quantise_v(1, s - 4)
+            if s == 5:
+                for r in range(2):
+                    attend(r, other_psum)
+                    divide(r)
+
+        energy(LAST, 0, 0, BANK)
+        maximum(LAST, 0)
+        energy(LAST, 1, 0, BANK)
         transpose_e(5)
         copy_e(5)
-        maximum(7, 1)
-        negate_maximum(7)
-        attend(2)
-        exponentials(7)
+        transpose_inverse(2)
+        transpose_inverse(3)
+        maximum(LAST, 1)
+        negate_maximum(LAST)
+        attend(2, energy_psum)
+        attend(3, energy_psum)
+        exponentials(LAST)
         transpose_e(6)
+        transpose_inverse(4)
         copy_e(6)
-        divide_columns(2)
-        quantise_e(5)
         denominator(6)
-        attend(3)
+        quantise_e(5)
+        divide(2)
         project(0, 0)
-        divide_columns(3)
+        divide(3)
         attend_by_points(5)
-        attend(4)
+        attend(4, energy_psum)
         quantise_ctx(2)
         quantise_ctx(3)
         add_and_store(0, 0)
         quantise_e(6)
-        denominator(7)
-        transpose_e(7)
-        divide_rows(5)
-        copy_e(7)
-        divide_columns(4)
+        divide(4)
         project(0, 1)
+        denominator(LAST)
+        transpose_e(LAST)
+        divide_by_points(5)
+        copy_e(LAST)
         attend_by_points(6)
         project(1, 0)
+        project(1, 1)
         add_and_store(0, 1)
-        divide_rows(6)
+        divide_by_points(6)
         transpose_ctx(5)
-        transpose_inverse(7)
+        transpose_inverse(LAST)
         copy_ctx(5)
         quantise_ctx(4)
-        quantise_e(7)
-        project(1, 1)
+        quantise_e(LAST)
         add_and_store(1, 0)
-        attend(7)
+        attend(LAST, energy_psum)
         add_and_store(1, 1)
         quantise_ctx(5)
-        divide_columns(7)
+        divide(LAST)
         transpose_ctx(6)
         copy_ctx(6)
         project(2, 0)
         project(2, 1)
         quantise_ctx(6)
-        quantise_ctx(7)
+        quantise_ctx(LAST)
         add_and_store(2, 0)
         project(3, 0)
         project(3, 1)

@@ -65,14 +65,12 @@ def tile_i2p_crossattention_pa_kernel(tc, q, k, v, Wo_words, Wo_scales, bo, feat
         make_identity(nc, identity[:])
 
         def load_rows(rows, source, first, count):
-            tiles = slice(first, first + count)
-            nc.sync.dma_start(out=rows[:, tiles, :], in_=source.rearrange("(a p) c -> p a c", p=P)[:, tiles, :])
+            chunk = source[first * P : (first + count) * P, :].rearrange("(p a) c -> p a c", a=count)
+            nc.sync.dma_start(out=rows[:, first : first + count, :], in_=chunk)
 
-        def load_first_q_and_k(b):
-            load_rows(q_rows[b], q[b], 0, 1)
+        def load_k(b):
             for tile in range(0, POSITION_TILES, 2):
                 load_rows(k_rows[b], k[b], tile, 2)
-            load_rows(q_rows[b], q[b], 1, 1)
 
         def load_v(b, g):
             positions = slice(g * P * PACK, (g + 1) * P * PACK)
@@ -84,12 +82,15 @@ def tile_i2p_crossattention_pa_kernel(tc, q, k, v, Wo_words, Wo_scales, bo, feat
         def load_feat(b):
             nc.sync.dma_start(out=feat[b][:], in_=feat0[b].rearrange("(o p) n -> p o n", p=P))
 
-        load_first_q_and_k(0)
+        load_rows(q_rows[0], q[0], 0, 1)
+        load_k(0)
+        load_rows(q_rows[0], q[0], 1, 1)
         load_v(0, 0)
         load_rows(q_rows[0], q[0], 2, 2)
         nc.sync.dma_start(out=bias_rows[0:OUT_TILES, :], in_=bo.rearrange("(o p) -> o p", p=P))
         load_v(0, 1)
-        load_first_q_and_k(1)
+        load_rows(q_rows[1], q[1], 0, 2)
+        load_k(1)
         load_rows(q_rows[1], q[1], 2, 2)
         load_v(1, 0)
         load_v(1, 1)
@@ -116,20 +117,21 @@ def tile_i2p_crossattention_pa_kernel(tc, q, k, v, Wo_words, Wo_scales, bo, feat
             nc.tensor.transpose(bank[:], bias_rows_f32[:], identity[:])
             nc.vector.tensor_copy(out=bias[:], in_=bank[:, 0:OUT_TILES])
 
-        def transpose_rows(rows, transposed, first, count, copy, pool):
+        def transpose_rows(rows, transposed, first, count, words, copy, pool):
             tag = "energy" if pool is energy_psum else "other"
-            bank = pool.tile([P, 2, count * P], F32, name="rows_bank", tag=tag)
-            for a in range(count):
-                words = rows[:, first + a, :].bitcast(F32)
-                for w in range(2):
-                    nc.tensor.transpose(bank[:, w, a * P : (a + 1) * P], words[:, w * P : (w + 1) * P], identity[:])
-            copy(out=transposed[:].bitcast(F32)[:, :, first * P : (first + count) * P], in_=bank[:])
+            bank = pool.tile([P, len(words), count, P], F32, name="rows_bank", tag=tag)
+            for x, w in enumerate(words):
+                for a in range(count):
+                    source = rows[:, first + a, :].bitcast(F32)[:, w * P : (w + 1) * P]
+                    nc.tensor.transpose(bank[:, x, a, :], source, identity[:])
+            target = transposed[:].bitcast(F32)[:, words[0] : words[-1] + 1, first * P : (first + count) * P]
+            copy(out=target.rearrange("p w (r a) -> p w r a", a=count), in_=bank[:].rearrange("p w a r -> p w r a"))
 
         def transpose_q(b, first, count, copy):
-            transpose_rows(q_rows[b], q_t[b], first, count, copy, other_psum)
+            transpose_rows(q_rows[b], q_t[b], first, count, (0, 1), copy, other_psum)
 
-        def transpose_k(b, first, count, copy, pool):
-            transpose_rows(k_rows[b], k_t[b], first, count, copy, pool)
+        def transpose_k(b, first, words, copy, pool):
+            transpose_rows(k_rows[b], k_t[b], first, 2, words, copy, pool)
 
         def energy(s, h, start, stop):
             b, i = divmod(s, POINT_TILES)
@@ -324,15 +326,14 @@ def tile_i2p_crossattention_pa_kernel(tc, q, k, v, Wo_words, Wo_scales, bo, feat
             multiply_zeros(BANK)
         transpose_q(0, 0, 1, scalar_copy)
         multiply_zeros(KEEP_WARM)
-        for tile in range(POSITION_TILES):
-            transpose_k(
-                0, tile, 1, vector_copy if tile % 2 == 0 else scalar_copy, energy_psum if tile in (0, 2) else other_psum
-            )
-            if tile in (1, 3):
+        for tile in range(0, POSITION_TILES, 2):
+            transpose_k(0, tile, (0,), vector_copy, energy_psum if tile < 4 else other_psum)
+            transpose_k(0, tile, (1,), scalar_copy, other_psum)
+            if tile < 4:
                 multiply_zeros(KEEP_WARM)
-            if tile == 5:
+            if tile == 4:
                 energy(0, 0, 0, PAIR)
-            if tile == 7:
+            if tile == 6:
                 energy(0, 0, PAIR, BANK)
         transpose_q(0, 1, 1, scalar_copy)
         energy(0, 1, 0, PAIR)
@@ -353,13 +354,12 @@ def tile_i2p_crossattention_pa_kernel(tc, q, k, v, Wo_words, Wo_scales, bo, feat
             if s == 1:
                 transpose_bias()
             if s == 2:
-                transpose_q(1, 0, 1, scalar_copy)
-                transpose_k(1, 0, 2, vector_copy, other_psum)
-                transpose_k(1, 2, 2, scalar_copy, other_psum)
+                transpose_q(1, 0, 2, scalar_copy)
+                transpose_k(1, 0, (0, 1), vector_copy, other_psum)
+                transpose_k(1, 2, (0, 1), scalar_copy, other_psum)
             if s == 3:
-                transpose_k(1, 4, 2, vector_copy, other_psum)
-                transpose_k(1, 6, 2, scalar_copy, other_psum)
-                transpose_q(1, 1, 1, vector_copy)
+                transpose_k(1, 4, (0, 1), vector_copy, other_psum)
+                transpose_k(1, 6, (0, 1), scalar_copy, other_psum)
             if s == 4:
                 transpose_q(1, 2, 2, vector_copy)
             for r in ready:

@@ -199,6 +199,21 @@ def tile_i2p_crossattention_pa_kernel(tc, q, k, v, Wo_words, Wo_scales, bo, feat
                 in_=e_banks[s][:].rearrange("p g u n -> p g n u"),
             )
 
+        def transpose_e_half(s, g):
+            e_banks[(s, g)] = other_psum.tile([P, 2, P], F32, name="e_half_bank", tag="other")
+            words = e_rows[s][:].bitcast(F32)
+            for u in range(2):
+                c = 2 * g + u
+                nc.tensor.transpose(e_banks[(s, g)][:, u, :], words[:, c * P : (c + 1) * P], identity[:])
+
+        def copy_e_half(s, g):
+            if g == 0:
+                e_grouped[s] = work.tile([P, PASSES, PACK * P], BF16, name="e_grouped", align_bytes=64)
+            nc.scalar.copy(
+                out=e_grouped[s][:, g].bitcast(F32).rearrange("p (n u) -> p n u", u=2),
+                in_=e_banks[(s, g)][:].rearrange("p u n -> p n u"),
+            )
+
         def quantise_e(s):
             e_codes[s] = lagged.tile([P, PASSES, P], U32, name="e_codes", align_bytes=64)
             e_scales[s] = lagged.tile([P, PASSES, P], U8, name="e_scales", align_bytes=64)
@@ -329,9 +344,9 @@ def tile_i2p_crossattention_pa_kernel(tc, q, k, v, Wo_words, Wo_scales, bo, feat
         for tile in range(0, POSITION_TILES, 2):
             transpose_k(0, tile, (0,), vector_copy, energy_psum if tile < 4 else other_psum)
             transpose_k(0, tile, (1,), scalar_copy, other_psum)
-            if tile < 4:
+            if tile < 2:
                 multiply_zeros(KEEP_WARM)
-            if tile == 4:
+            if tile == 2:
                 energy(0, 0, 0, PAIR)
             if tile == 6:
                 energy(0, 0, PAIR, BANK)
@@ -412,31 +427,33 @@ def tile_i2p_crossattention_pa_kernel(tc, q, k, v, Wo_words, Wo_scales, bo, feat
         project(0, 0)
         divide(3)
         attend_by_points(5)
+        divide_by_points(5)
         attend(4, energy_psum)
         quantise_ctx(2)
         quantise_ctx(3)
         add_and_store(0, 0)
+        denominator(LAST)
         quantise_e(6)
         divide(4)
         project(0, 1)
-        denominator(LAST)
-        transpose_e(LAST)
-        divide_by_points(5)
-        copy_e(LAST)
+        transpose_e_half(LAST, 0)
+        transpose_e_half(LAST, 1)
+        transpose_ctx(5)
+        copy_e_half(LAST, 0)
+        copy_e_half(LAST, 1)
+        copy_ctx(5)
         attend_by_points(6)
         project(1, 0)
         project(1, 1)
         add_and_store(0, 1)
         divide_by_points(6)
-        transpose_ctx(5)
-        transpose_inverse(LAST)
-        copy_ctx(5)
         quantise_ctx(4)
         quantise_e(LAST)
+        transpose_inverse(LAST)
         add_and_store(1, 0)
         attend(LAST, energy_psum)
-        add_and_store(1, 1)
         quantise_ctx(5)
+        add_and_store(1, 1)
         divide(LAST)
         transpose_ctx(6)
         copy_ctx(6)

@@ -46,8 +46,8 @@ def tile_i2p_crossattention_pa_kernel(tc, q, k, v, Wo_words, Wo_scales, bo, feat
         bias_rows = keep.tile([P, P], BF16, name="bias_rows")
         bias_rows_f32 = keep.tile([P, P], F32, name="bias_rows_f32")
         bias = keep.tile([P, OUT_TILES], F32, name="bias")
-        w_codes = keep.tile([P, CHANNELS], U32, name="w_codes", align_bytes=64)
-        w_scales = keep.tile([P, CHANNELS], U8, name="w_scales", align_bytes=64)
+        w_codes = keep.tile([P, CHANNELS], U32, name="w_codes", align_bytes=256)
+        w_scales = keep.tile([P, CHANNELS], U8, name="w_scales", align_bytes=256)
         q_rows, k_rows, v_rows, feat, q_t, k_t, v_codes, v_scales = [], [], [], [], [], [], [], []
         for b in range(BATCH):
             q_rows.append(keep.tile([P, POINT_TILES, CHANNELS], BF16, name="q_rows%d" % b))
@@ -56,8 +56,8 @@ def tile_i2p_crossattention_pa_kernel(tc, q, k, v, Wo_words, Wo_scales, bo, feat
             v_rows.append(keep.tile([P, PASSES, PACK, CHANNELS], BF16, name="v_rows%d" % b))
             q_t.append(keep.tile([P, 2, 2 * POINTS], BF16, name="q_t%d" % b))
             k_t.append(keep.tile([P, 2, 2 * POSITIONS], BF16, name="k_t%d" % b))
-            v_codes.append(keep.tile([P, PASSES, CHANNELS], U32, name="v_codes%d" % b, align_bytes=64))
-            v_scales.append(keep.tile([P, PASSES, CHANNELS], U8, name="v_scales%d" % b, align_bytes=64))
+            v_codes.append(keep.tile([P, PASSES, CHANNELS], U32, name="v_codes%d" % b, align_bytes=256))
+            v_scales.append(keep.tile([P, PASSES, CHANNELS], U8, name="v_scales%d" % b, align_bytes=256))
 
         nc.vector.memset(warm[:], 0.0)
         nc.vector.memset(w_scales[:].bitcast(I32), 0)
@@ -215,8 +215,8 @@ def tile_i2p_crossattention_pa_kernel(tc, q, k, v, Wo_words, Wo_scales, bo, feat
             )
 
         def quantise_e(s):
-            e_codes[s] = lagged.tile([P, PASSES, P], U32, name="e_codes", align_bytes=64)
-            e_scales[s] = lagged.tile([P, PASSES, P], U8, name="e_scales", align_bytes=64)
+            e_codes[s] = lagged.tile([P, PASSES, P], U32, name="e_codes", align_bytes=256)
+            e_scales[s] = lagged.tile([P, PASSES, P], U8, name="e_scales", align_bytes=256)
             nc.vector.quantize_mx(
                 out=e_codes[s][:].rearrange("p g n -> p (g n)").bitcast(FP8X4),
                 scales=e_scales[s][:].rearrange("p g n -> p (g n)"),
@@ -300,8 +300,8 @@ def tile_i2p_crossattention_pa_kernel(tc, q, k, v, Wo_words, Wo_scales, bo, feat
         def quantise_ctx(s):
             pair, member = divmod(s, 2)
             if member == 0:
-                ctx_codes[pair] = lagged.tile([P, PAIR], U32, name="ctx_codes", align_bytes=64)
-                ctx_scales[pair] = lagged.tile([P, PAIR], U8, name="ctx_scales", align_bytes=64)
+                ctx_codes[pair] = lagged.tile([P, PAIR], U32, name="ctx_codes", align_bytes=256)
+                ctx_scales[pair] = lagged.tile([P, PAIR], U8, name="ctx_scales", align_bytes=256)
             points = slice(member * P, (member + 1) * P)
             nc.vector.quantize_mx(
                 out=ctx_codes[pair][:, points].bitcast(FP8X4),

import math
from contextlib import ExitStack

import concourse.mybir as mybir
from concourse.masks import make_identity

F32 = mybir.dt.float32
BF16 = mybir.dt.bfloat16
I32 = mybir.dt.int32
U32 = mybir.dt.uint32
U8 = mybir.dt.uint8
FP8X4 = mybir.dt.float8_e4m3fn_x4
ALU = mybir.AluOpType
ACT = mybir.ActivationFunctionType
AXIS = mybir.AxisListType

P = 128
PACK = 4
BANK = 512
BATCH, POINTS, POSITIONS, CHANNELS = 2, 512, 1024, 512
POINT_TILES = POINTS // P
STEPS = BATCH * POINT_TILES
LAST = STEPS - 1
HALVES = POSITIONS // BANK
PASSES = POSITIONS // (P * PACK)
OUT_TILES = CHANNELS // P
POSITION_TILES = POSITIONS // P
PAIR = 2 * P
KEEP_WARM = 384
FLOPS = 2 * BATCH * (2 * POINTS * POSITIONS * CHANNELS + POINTS * CHANNELS * CHANNELS)


def tile_i2p_crossattention_pa_kernel(tc, q, k, v, Wo_words, Wo_scales, bo, feat0, out):
    nc = tc.nc
    with ExitStack() as ctx:
        ctx.enter_context(tc.manual_schedule())
        keep = ctx.enter_context(tc.tile_pool(name="keep", bufs=1))
        small = ctx.enter_context(tc.tile_pool(name="small", bufs=3))
        work = ctx.enter_context(tc.tile_pool(name="work", bufs=2))
        lagged = ctx.enter_context(tc.tile_pool(name="lagged", bufs=STEPS))
        energy_psum = ctx.enter_context(tc.psum_pool(name="energy_psum", bufs=4))
        other_psum = ctx.enter_context(tc.psum_pool(name="other_psum", bufs=4))

        identity = keep.tile([P, P], F32, name="identity")
        warm = keep.tile([P, BANK], BF16, name="warm")
        bias_rows = keep.tile([P, P], BF16, name="bias_rows")
        bias_rows_f32 = keep.tile([P, P], F32, name="bias_rows_f32")
        bias = keep.tile([P, OUT_TILES], F32, name="bias")
        w_codes = keep.tile([P, CHANNELS], U32, name="w_codes", align_bytes=256)
        w_scales = keep.tile([P, CHANNELS], U8, name="w_scales", align_bytes=256)
        q_rows, k_rows, v_rows, feat, q_t, k_t, v_codes, v_scales = [], [], [], [], [], [], [], []
        for b in range(BATCH):
            q_rows.append(keep.tile([P, POINT_TILES, CHANNELS], BF16, name="q_rows%d" % b))
            k_rows.append(keep.tile([P, POSITION_TILES, CHANNELS], BF16, name="k_rows%d" % b))
            feat.append(keep.tile([P, OUT_TILES, POINTS], BF16, name="feat%d" % b))
            v_rows.append(keep.tile([P, PASSES, PACK, CHANNELS], BF16, name="v_rows%d" % b))
            q_t.append(keep.tile([P, 2, 2 * POINTS], BF16, name="q_t%d" % b))
            k_t.append(keep.tile([P, 2, 2 * POSITIONS], BF16, name="k_t%d" % b))
            v_codes.append(keep.tile([P, PASSES, CHANNELS], U32, name="v_codes%d" % b, align_bytes=256))
            v_scales.append(keep.tile([P, PASSES, CHANNELS], U8, name="v_scales%d" % b, align_bytes=256))

        nc.vector.memset(warm[:], 0.0)
        nc.vector.memset(w_scales[:].bitcast(I32), 0)
        nc.vector.memset(bias_rows[:], 0.0)
        make_identity(nc, identity[:])

        def load_rows(rows, source, first, count):
            chunk = source[first * P : (first + count) * P, :].rearrange("(p a) c -> p a c", a=count)
            nc.sync.dma_start(out=rows[:, first : first + count, :], in_=chunk)

        def load_k(b):
            for tile in range(0, POSITION_TILES, 2):
                load_rows(k_rows[b], k[b], tile, 2)

        def load_v(b, g):
            positions = slice(g * P * PACK, (g + 1) * P * PACK)
            nc.sync.dma_start(
                out=v_rows[b][:, g].rearrange("p (u j) c -> p u (j c)", j=2),
                in_=v[b, positions, :].rearrange("(u p j) c -> p u (j c)", u=2, j=2),
            )

        def load_feat(b):
            nc.sync.dma_start(out=feat[b][:], in_=feat0[b].rearrange("(o p) n -> p o n", p=P))

        load_rows(q_rows[0], q[0], 0, 1)
        load_k(0)
        load_rows(q_rows[0], q[0], 1, 1)
        load_v(0, 0)
        load_rows(q_rows[0], q[0], 2, 2)
        nc.sync.dma_start(out=bias_rows[0:OUT_TILES, :], in_=bo.rearrange("(o p) -> o p", p=P))
        load_v(0, 1)
        load_rows(q_rows[1], q[1], 0, 2)
        load_k(1)
        load_rows(q_rows[1], q[1], 2, 2)
        load_v(1, 0)
        load_v(1, 1)
        nc.sync.dma_start(out=w_codes[:].bitcast(I32), in_=Wo_words[0].rearrange("p n t -> p (n t)").bitcast(I32))
        for quadrant in range(4):
            nc.sync.dma_start(
                out=w_scales[32 * quadrant : 32 * quadrant + 4, :].bitcast(I32),
                in_=Wo_scales[0, 4 * quadrant : 4 * quadrant + 4, :].bitcast(I32),
            )
        load_feat(0)
        load_feat(1)

        warm_bank = energy_psum.tile([P, BANK], F32, name="warm_bank", tag="energy")

        def multiply_zeros(columns):
            nc.tensor.matmul(warm_bank[:, 0:columns], lhsT=warm[:, 0:P], rhs=warm[:, 0:columns], start=True, stop=True)

        energy_banks, row_max, neg_maxima, row_sums, inverses = {}, {}, {}, {}, {}
        e_rows, e_banks, e_grouped, e_codes, e_scales, v_grouped = {}, {}, {}, {}, {}, {}
        inv_cols, ctx_banks, ctx_rows, ctx_grouped, ctx_codes, ctx_scales, y_banks = {}, {}, {}, {}, {}, {}, {}

        def transpose_bias():
            bank = other_psum.tile([P, P], F32, name="bias_bank", tag="other")
            nc.tensor.transpose(bank[:], bias_rows_f32[:], identity[:])
            nc.vector.tensor_copy(out=bias[:], in_=bank[:, 0:OUT_TILES])

        def transpose_rows(rows, transposed, first, count, words, copy, pool):
            tag = "energy" if pool is energy_psum else "other"
            bank = pool.tile([P, len(words), count, P], F32, name="rows_bank", tag=tag)
            for x, w in enumerate(words):
                for a in range(count):
                    source = rows[:, first + a, :].bitcast(F32)[:, w * P : (w + 1) * P]
                    nc.tensor.transpose(bank[:, x, a, :], source, identity[:])
            target = transposed[:].bitcast(F32)[:, words[0] : words[-1] + 1, first * P : (first + count) * P]
            copy(out=target.rearrange("p w (r a) -> p w r a", a=count), in_=bank[:].rearrange("p w a r -> p w r a"))

        def transpose_q(b, first, count, copy):
            transpose_rows(q_rows[b], q_t[b], first, count, (0, 1), copy, other_psum)

        def transpose_k(b, first, words, copy, pool):
            transpose_rows(k_rows[b], k_t[b], first, 2, words, copy, pool)

        def energy(s, h, start, stop):
            b, i = divmod(s, POINT_TILES)
            q_view = q_t[b][:].rearrange("p w (r j) -> p w r j", j=2)
            k_view = k_t[b][:].rearrange("p w (r j) -> p w r j", j=2)
            if start == 0:
                energy_banks[(s, h)] = energy_psum.tile([P, BANK], F32, name="energy_bank", tag="energy")
            for c in range(4):
                w, j = divmod(c, 2)
                nc.tensor.matmul(
                    energy_banks[(s, h)][:, start:stop],
                    lhsT=q_view[:, w, i * P : (i + 1) * P, j],
                    rhs=k_view[:, w, h * BANK + start : h * BANK + stop, j],
                    start=(c == 0),
                    stop=(c == 3),
                )

        def maximum(s, h):
            if h == 0:
                row_max[s] = small.tile([P, HALVES], F32, name="row_max")
            nc.vector.reduce_max(out=row_max[s][:, h : h + 1], in_=energy_banks[(s, h)][:], axis=AXIS.X)

        def negate_maximum(s):
            neg_maxima[s] = small.tile([P, 1], F32, name="neg_max")
            nc.vector.tensor_scalar(
                out=neg_maxima[s][:], in0=row_max[s][:, 0:1], scalar1=row_max[s][:, 1:2], scalar2=-1.0,
                op0=ALU.max, op1=ALU.mult,
            )

        def exponentials(s):
            e_rows[s] = lagged.tile([P, POSITIONS], BF16, name="e_rows")
            row_sums[s] = small.tile([P, HALVES], F32, name="row_sums")
            for h in range(HALVES):
                nc.scalar.activation(
                    out=e_rows[s][:, h * BANK : (h + 1) * BANK], in_=energy_banks[(s, h)][:], func=ACT.Exp,
                    bias=neg_maxima[s][:], scale=1.0, accum_out=row_sums[s][:, h : h + 1],
                )

        def denominator(s):
            scaled_sum = small.tile([P, 1], F32, name="scaled_sum")
            nc.gpsimd.tensor_scalar(
                out=scaled_sum[:], in0=row_sums[s][:, 0:1], scalar1=row_sums[s][:, 1:2],
                scalar2=math.sqrt(CHANNELS), op0=ALU.add, op1=ALU.mult,
            )
            inverses[s] = lagged.tile([P, 1], F32, name="inverse")
            nc.vector.reciprocal(out=inverses[s][:], in_=scaled_sum[:])

        def transpose_inverse(s):
            bank = other_psum.tile([P, P], F32, name="inv_bank", tag="other")
            nc.tensor.transpose(bank[:], inverses[s][:, 0:1].to_broadcast([P, P]), identity[:])
            inv_cols[s] = lagged.tile([P, P], F32, name="inv_cols")
            nc.scalar.copy(out=inv_cols[s][:], in_=bank[:])

        def transpose_e(s):
            e_banks[s] = other_psum.tile([P, PASSES, 2, P], F32, name="e_bank", tag="other")
            words = e_rows[s][:].bitcast(F32)
            for c in range(2 * PASSES):
                g, u = divmod(c, 2)
                nc.tensor.transpose(e_banks[s][:, g, u, :], words[:, c * P : (c + 1) * P], identity[:])

        def copy_e(s):
            e_grouped[s] = work.tile([P, PASSES, PACK * P], BF16, name="e_grouped", align_bytes=64)
            nc.scalar.copy(
                out=e_grouped[s][:].bitcast(F32).rearrange("p g (n u) -> p g n u", u=2),
                in_=e_banks[s][:].rearrange("p g u n -> p g n u"),
            )

        def transpose_e_half(s, g):
            e_banks[(s, g)] = other_psum.tile([P, 2, P], F32, name="e_half_bank", tag="other")
            words = e_rows[s][:].bitcast(F32)
            for u in range(2):
                c = 2 * g + u
                nc.tensor.transpose(e_banks[(s, g)][:, u, :], words[:, c * P : (c + 1) * P], identity[:])

        def copy_e_half(s, g):
            if g == 0:
                e_grouped[s] = work.tile([P, PASSES, PACK * P], BF16, name="e_grouped", align_bytes=64)
            nc.scalar.copy(
                out=e_grouped[s][:, g].bitcast(F32).rearrange("p (n u) -> p n u", u=2),
                in_=e_banks[(s, g)][:].rearrange("p u n -> p n u"),
            )

        def quantise_e(s):
            e_codes[s] = lagged.tile([P, PASSES, P], U32, name="e_codes", align_bytes=256)
            e_scales[s] = lagged.tile([P, PASSES, P], U8, name="e_scales", align_bytes=256)
            nc.vector.quantize_mx(
                out=e_codes[s][:].rearrange("p g n -> p (g n)").bitcast(FP8X4),
                scales=e_scales[s][:].rearrange("p g n -> p (g n)"),
                in_=e_grouped[s][:].rearrange("p g c -> p (g c)"),
            )

        def regroup_v(b, g):
            v_grouped[(b, g)] = work.tile([P, PACK, P, PACK], BF16, name="v_grouped", align_bytes=64)
            source = v_rows[b][:, g].rearrange("p row (i t) -> p i row t", t=PACK)
            target = v_grouped[(b, g)][:].rearrange("p t i row -> p i row t")
            nc.vector.tensor_copy(out=target[:, 0 : P // 2], in_=source[:, 0 : P // 2])
            nc.scalar.copy(out=target[:, P // 2 : P], in_=source[:, P // 2 : P])

        def quantise_v(b, g):
            nc.vector.quantize_mx(
                out=v_codes[b][:, g, :].bitcast(FP8X4),
                scales=v_scales[b][:, g, :],
                in_=v_grouped[(b, g)][:].rearrange("p t i row -> p (t i row)"),
            )

        def attend(s, pool):
            b = s // POINT_TILES
            tag = "energy" if pool is energy_psum else "other"
            ctx_banks[s] = pool.tile([P, PACK, P], F32, name="ctx_bank", tag=tag)
            for t in range(PACK):
                channels = slice(t * P, (t + 1) * P)
                for g in range(PASSES):
                    nc.tensor.matmul_mx(
                        out=ctx_banks[s][:, t, :],
                        lhsT=v_codes[b][:, g, channels].bitcast(FP8X4),
                        lhsT_scale=v_scales[b][:, g, channels],
                        rhs=e_codes[s][:, g, :].bitcast(FP8X4),
                        rhs_scale=e_scales[s][:, g, :],
                        start=(g == 0),
                        stop=(g == PASSES - 1),
                    )

        def divide(s):
            ctx_grouped[s] = lagged.tile([P, P, PACK], BF16, name="ctx_grouped", align_bytes=64)
            nc.vector.tensor_tensor(
                out=ctx_grouped[s][:],
                in0=ctx_banks[s][:].rearrange("p t n -> p n t"),
                in1=inv_cols[s][:].unsqueeze(2).to_broadcast([P, P, PACK]),
                op=ALU.mult,
            )

        def attend_by_points(s):
            b = s // POINT_TILES
            ctx_banks[s] = energy_psum.tile([P, CHANNELS], F32, name="ctx_rows_bank", tag="energy")
            for g in range(PASSES):
                nc.tensor.matmul_mx(
                    out=ctx_banks[s][:],
                    lhsT=e_codes[s][:, g, :].bitcast(FP8X4),
                    lhsT_scale=e_scales[s][:, g, :],
                    rhs=v_codes[b][:, g, :].bitcast(FP8X4),
                    rhs_scale=v_scales[b][:, g, :],
                    start=(g == 0),
                    stop=(g == PASSES - 1),
                )

        def divide_by_points(s):
            ctx_rows[s] = work.tile([P, 2, P, 2], BF16, name="ctx_rows")
            nc.scalar.activation(
                out=ctx_rows[s][:], in_=ctx_banks[s][:].rearrange("n (u j i) -> n u i j", u=2, j=2), func=ACT.Copy,
                scale=inverses[s][:, 0:1],
            )

        def transpose_ctx(s):
            ctx_banks[s] = other_psum.tile([P, 2, P], F32, name="ctx_t_bank", tag="other")
            words = ctx_rows[s][:].rearrange("n u i j -> n (u i j)").bitcast(F32)
            for u in range(2):
                nc.tensor.transpose(ctx_banks[s][:, u, :], words[:, u * P : (u + 1) * P], identity[:])

        def copy_ctx(s):
            ctx_grouped[s] = lagged.tile([P, P, PACK], BF16, name="ctx_grouped", align_bytes=64)
            nc.scalar.copy(
                out=ctx_grouped[s][:].rearrange("p n t -> p (n t)").bitcast(F32).rearrange("p (n u) -> p n u", u=2),
                in_=ctx_banks[s][:].rearrange("p u n -> p n u"),
            )

        def quantise_ctx(s):
            pair, member = divmod(s, 2)
            if member == 0:
                ctx_codes[pair] = lagged.tile([P, PAIR], U32, name="ctx_codes", align_bytes=256)
                ctx_scales[pair] = lagged.tile([P, PAIR], U8, name="ctx_scales", align_bytes=256)
            points = slice(member * P, (member + 1) * P)
            nc.vector.quantize_mx(
                out=ctx_codes[pair][:, points].bitcast(FP8X4),
                scales=ctx_scales[pair][:, points],
                in_=ctx_grouped[s][:].rearrange("p n t -> p (n t)"),
            )

        def project(pair, part):
            y_banks[(pair, part)] = other_psum.tile([P, 2, PAIR], F32, name="y_bank", tag="other")
            for c in range(2):
                o = 2 * part + c
                nc.tensor.matmul_mx(
                    out=y_banks[(pair, part)][:, c, :],
                    lhsT=w_codes[:, o * P : (o + 1) * P].bitcast(FP8X4),
                    lhsT_scale=w_scales[:, o * P : (o + 1) * P],
                    rhs=ctx_codes[pair][:].bitcast(FP8X4),
                    rhs_scale=ctx_scales[pair][:],
                    start=True,
                    stop=True,
                )

        def add_and_store(pair, part):
            b, place = divmod(pair, POINTS // PAIR)
            points = slice(place * PAIR, (place + 1) * PAIR)
            result = lagged.tile([P, 2, PAIR], F32, name="result")
            for c in range(2):
                o = 2 * part + c
                nc.vector.scalar_tensor_tensor(
                    out=result[:, c, :], in0=y_banks[(pair, part)][:, c, :], scalar=bias[:, o : o + 1],
                    in1=feat[b][:, o, points], op0=ALU.add, op1=ALU.add,
                )
                nc.sync.dma_start(out=out[b, o * P : (o + 1) * P, points], in_=result[:, c, :])

        scalar_copy, vector_copy = nc.scalar.copy, nc.vector.tensor_copy

        for count in range(4):
            multiply_zeros(BANK)
        transpose_q(0, 0, 1, scalar_copy)
        multiply_zeros(KEEP_WARM)
        for tile in range(0, POSITION_TILES, 2):
            transpose_k(0, tile, (0,), vector_copy, energy_psum if tile < 4 else other_psum)
            transpose_k(0, tile, (1,), scalar_copy, other_psum)
            if tile < 2:
                multiply_zeros(KEEP_WARM)
            if tile == 2:
                energy(0, 0, 0, PAIR)
            if tile == 6:
                energy(0, 0, PAIR, BANK)
        transpose_q(0, 1, 1, scalar_copy)
        energy(0, 1, 0, PAIR)
        maximum(0, 0)
        regroup_v(0, 0)
        energy(0, 1, PAIR, BANK)
        transpose_q(0, 2, 2, scalar_copy)
        maximum(0, 1)
        nc.vector.tensor_copy(out=bias_rows_f32[:], in_=bias_rows[:])
        negate_maximum(0)
        exponentials(0)
        quantise_v(0, 0)

        for s in range(1, LAST):
            ready = (0,) if s == 3 else (s - 3, s - 2) if s in (4, 6) else ()
            energy(s, 0, 0, BANK)
            maximum(s, 0)
            if s == 1:
                transpose_bias()
            if s == 2:
                transpose_q(1, 0, 2, scalar_copy)
                transpose_k(1, 0, (0, 1), vector_copy, other_psum)
                transpose_k(1, 2, (0, 1), scalar_copy, other_psum)
            if s == 3:
                transpose_k(1, 4, (0, 1), vector_copy, other_psum)
                transpose_k(1, 6, (0, 1), scalar_copy, other_psum)
            if s == 4:
                transpose_q(1, 2, 2, vector_copy)
            for r in ready:
                transpose_e(r)
                copy_e(r)
            if s == 5:
                transpose_inverse(0)
                transpose_inverse(1)
            if s == 1:
                regroup_v(0, 1)
            if s in (3, 4):
                regroup_v(1, s - 3)
            energy(s, 1, 0, BANK)
            maximum(s, 1)
            if s == 6:
                quantise_ctx(0)
                quantise_ctx(1)
            negate_maximum(s)
            exponentials(s)
            denominator(s - 1)
            for r in ready:
                quantise_e(r)
            if s == 2:
                quantise_v(0, 1)
            if s in (4, 5):
                quantise_v(1, s - 4)
            if s == 5:
                for r in range(2):
                    attend(r, other_psum)
                    divide(r)

        energy(LAST, 0, 0, BANK)
        maximum(LAST, 0)
        energy(LAST, 1, 0, BANK)
        transpose_e(5)
        copy_e(5)
        transpose_inverse(2)
        transpose_inverse(3)
        maximum(LAST, 1)
        negate_maximum(LAST)
        attend(2, energy_psum)
        attend(3, energy_psum)
        exponentials(LAST)
        transpose_e(6)
        transpose_inverse(4)
        copy_e(6)
        denominator(6)
        quantise_e(5)
        divide(2)
        project(0, 0)
        divide(3)
        attend_by_points(5)
        divide_by_points(5)
        attend(4, energy_psum)
        quantise_ctx(2)
        quantise_ctx(3)
        add_and_store(0, 0)
        denominator(LAST)
        quantise_e(6)
        divide(4)
        project(0, 1)
        transpose_e_half(LAST, 0)
        transpose_e_half(LAST, 1)
        transpose_ctx(5)
        copy_e_half(LAST, 0)
        copy_e_half(LAST, 1)
        copy_ctx(5)
        attend_by_points(6)
        project(1, 0)
        project(1, 1)
        add_and_store(0, 1)
        divide_by_points(6)
        quantise_ctx(4)
        quantise_e(LAST)
        transpose_inverse(LAST)
        add_and_store(1, 0)
        attend(LAST, energy_psum)
        quantise_ctx(5)
        add_and_store(1, 1)
        divide(LAST)
        transpose_ctx(6)
        copy_ctx(6)
        project(2, 0)
        project(2, 1)
        quantise_ctx(6)
        quantise_ctx(LAST)
        add_and_store(2, 0)
        project(3, 0)
        project(3, 1)
        add_and_store(2, 1)
        add_and_store(3, 0)
        add_and_store(3, 1)
